import numpy as np
import ml_dtypes


def mxq(x, axis, fmt="e4m3"):
    dtype, down = {"e4m3": (ml_dtypes.float8_e4m3fn, 7), "e5m2": (ml_dtypes.float8_e5m2, 14)}[fmt]
    v = np.moveaxis(np.asarray(x, np.float32).astype(ml_dtypes.bfloat16).astype(np.float64), axis, -1)
    blocks = v.reshape(v.shape[:-1] + (-1, 32))
    amax = np.abs(blocks).max(-1, keepdims=True)
    byte = np.maximum(np.where(amax > 0, np.frexp(amax)[1] - 1 + 127, 0) - down, 1)
    scale = np.exp2(byte - 127.0)
    codes = (blocks / scale).astype(np.float32).astype(dtype).astype(np.float64)
    return np.moveaxis((codes * scale).reshape(v.shape), -1, axis)


WIDE = False


def mx_kscale(k):
    if not WIDE:
        return np.ones(k)
    levels = np.array([18, -18])
    if k % 512:
        return np.exp2(np.random.permutation(np.resize(levels, k // 32))).repeat(32)
    a = np.empty((k // 512, 16))
    for p in range(k // 512):
        a[p, :8] = np.random.permutation(np.resize(levels, 8))
        for g in range(8):
            far = levels[np.abs(levels - a[p, g]) >= 10]
            a[p, g + 8] = far[np.random.randint(len(far))]
    return np.exp2(a.ravel()).repeat(32)


BF16 = ml_dtypes.bfloat16


def bf(x):
    return np.asarray(x, np.float32).astype(BF16)


def f64(x):
    return np.asarray(x).astype(np.float64)


B, S, DM, H, DH = 1, 1024, 1024, 8, 256
DI = H * DH
EPS_GN = 1e-5


def group_stats(h_attn):
    hg = f64(h_attn).reshape(B, S, H, DH)
    mu = hg.mean(axis=(1, 3))
    var = hg.var(axis=(1, 3))
    return mu, 1.0 / np.sqrt(var + EPS_GN)


def setup_inputs():
    t = np.maximum(mx_kscale(S), 1.0)[None, :, None]
    u = mx_kscale(DM)
    h = np.random.standard_normal((B, S, H, DH)) * 0.15 + np.random.standard_normal((B, 1, H, 1)) * 0.15
    h0 = bf(h.reshape(B, S, DI))
    gn_w = bf(1.0 + 0.1 * np.random.standard_normal(DI))
    gn_b = bf(0.1 * np.random.standard_normal(DI))
    w0 = bf(np.random.standard_normal((DM, DI)) / np.sqrt(DI))
    x = bf(np.random.standard_normal((B, S, DM)))
    skip_scale = bf(0.7 + 0.1 * np.random.standard_normal(1))
    g = np.random.standard_normal((B, S, DM)) * np.exp2(np.random.randint(-6, 1, (B, S, 1)))
    mu, rstd = group_stats(h0)
    return {"h_attn": bf(f64(h0) * t),
            "gn_w": gn_w,
            "gn_b": gn_b,
            "W_out": bf(f64(w0) / u[:, None]),
            "x": x,
            "skip_scale": skip_scale,
            "mu": np.asarray(mu, np.float32),
            "rstd": np.asarray(rstd, np.float32),
            "grad_out": bf(g / t * u)}


def reference(h_attn, gn_w, gn_b, W_out, x, skip_scale, mu, rstd, grad_out):
    m = f64(mu).reshape(B, 1, H, 1)
    r = f64(rstd).reshape(B, 1, H, 1)
    gw = f64(gn_w).reshape(H, DH)
    hn = (f64(h_attn).reshape(B, S, H, DH) - m) * r
    h = (hn * gw + f64(gn_b).reshape(H, DH)).reshape(B * S, DI)
    g = f64(grad_out).reshape(B * S, DM)
    dh = mxq(g, 1, "e5m2") @ mxq(f64(W_out), 0, "e4m3")
    dn = dh.reshape(B, S, H, DH) * gw
    m1 = dn.mean(axis=(1, 3), keepdims=True)
    m2 = (dn * hn).mean(axis=(1, 3), keepdims=True)
    dh_attn = (r * (dn - m1 - hn * m2)).reshape(B, S, DI)
    dW = mxq(g, 0, "e5m2").T @ mxq(h, 0, "e4m3")
    return dh_attn, dW

@@ -1,0 +1,411 @@
+from contextlib import ExitStack
+
+import concourse.mybir as mybir
+from concourse.masks import make_identity
+
+S, DM, H, DH = 1024, 1024, 8, 256
+DI = H * DH
+FLOPS = 2 * 2 * S * DM * DI
+BYTES = 2 * (S * DI + DM * DI + S * DM + 2 * DI) + 4 * 2 * H + 4 * (S * DI + DM * DI)
+
+F32 = mybir.dt.float32
+BF16 = mybir.dt.bfloat16
+U32 = mybir.dt.uint32
+U8 = mybir.dt.uint8
+E4 = mybir.dt.float8_e4m3fn_x4
+E5 = mybir.dt.float8_e5m2_x4
+ALU = mybir.AluOpType
+IDENT = mybir.ActivationFunctionType.Identity
+
+P = 128
+NB = DI // P
+CH = 512
+NC = DI // CH
+INV_N = 1.0 / (S * DH)
+BANKS = ["dh0", "dh1", "dw0", "dw1", "xt", "hw", "o0", "o1"]
+DW_ORDER = [3, 0, 1, 2]
+DW_FIRST = 2
+
+
+def tile_mlstmblock_pb_v_kernel(
+    tc, h_attn, gn_w, gn_b, W_out, x, skip_scale, mu, rstd, grad_out, out_0, out_1
+):
+    nc = tc.nc
+    xa = h_attn.rearrange("b (s q u) c -> q u (b s) c", q=P, u=2)
+    oa = out_0.rearrange("b (s q u) c -> q u (b s) c", q=P, u=2)
+    ga = grad_out.rearrange("b (g p j) d -> p (b g) j d", p=P, j=4)
+    wa = W_out.rearrange("(k p j) c -> p k j c", p=P, j=4)
+
+    with ExitStack() as ctx:
+        keep = ctx.enter_context(tc.tile_pool(name="keep", bufs=1))
+        work = ctx.enter_context(tc.tile_pool(name="work", bufs=2))
+        psum = ctx.enter_context(tc.psum_pool(name="psum", bufs=1))
+        ctx.enter_context(tc.manual_schedule())
+
+        def kept(name, shape, dtype):
+            return keep.tile(shape, dtype, name=name, tag=name, align_bytes=64)
+
+        def ring(name, shape, dtype, bufs):
+            return work.tile(shape, dtype, name=name, tag=name, bufs=bufs, align_bytes=64)
+
+        def bank(tag, shape, dtype):
+            return psum.tile(shape, dtype, name=tag, tag=tag)
+
+        wb_rows = kept("wb_rows", [P, P], BF16)
+        mr_col = kept("mr_col", [P, 8], F32)
+        nc.vector.memset(wb_rows[:], 0.0)
+        nc.vector.memset(mr_col[:], 0.0)
+        id_bf = kept("id_bf", [P, P], BF16)
+        id_f = kept("id_f", [P, P], F32)
+        make_identity(nc, id_bf[:])
+        make_identity(nc, id_f[:])
+        ones = kept("ones", [P, P], F32)
+        nc.scalar.activation(out=ones[:], in_=id_bf[:], func=IDENT, scale=0.0, bias=1.0)
+
+        nc.sync.dma_start(out=wb_rows[0:NB, :], in_=gn_w.rearrange("(b p) -> b p", p=P))
+        nc.sync.dma_start(out=wb_rows[NB : 2 * NB, :], in_=gn_b.rearrange("(b p) -> b p", p=P))
+        with nc.allow_non_contiguous_dma(reason="one float32 value to a partition"):
+            nc.sync.dma_start(out=mr_col[0:H, 0:1], in_=mu.rearrange("b h -> h b"))
+            nc.sync.dma_start(out=mr_col[H : 2 * H, 0:1], in_=rstd.rearrange("b h -> h b"))
+
+        x_sb, w_sb, g_sb = {}, {}, {}
+
+        def load_x(c):
+            for u in range(2):
+                x_sb[c, u] = kept("x%d%d" % (c, u), [P, 4, CH], BF16)
+                nc.sync.dma_start(out=x_sb[c, u][:], in_=xa[:, u, :, c * CH : (c + 1) * CH])
+
+        def load_w(c):
+            w_sb[c] = kept("w%d" % c, [P, 2, 4, CH], BF16)
+            for k in range(2):
+                nc.sync.dma_start(out=w_sb[c][:, k, :, :], in_=wa[:, k, :, c * CH : (c + 1) * CH])
+
+        def load_g(G):
+            for k in range(2):
+                g_sb[G, k] = kept("g%d%d" % (G, k), [P, 4, 512], BF16)
+                nc.sync.dma_start(out=g_sb[G, k][:], in_=ga[:, G, :, k * 512 : (k + 1) * 512])
+
+        load_x(3)
+        load_g(0)
+        load_w(0)
+        load_g(1)
+        load_x(0)
+        for c in range(1, 3):
+            load_w(c)
+            load_x(c)
+        load_w(3)
+
+        wb_ps = bank("o0", [P, P], BF16)
+        nc.tensor.transpose(wb_ps[:], wb_rows[:], id_bf[:])
+        mr_ps = bank("o1", [P, P], F32)
+        nc.tensor.transpose(mr_ps[:], mr_col[:, 0:1].to_broadcast([P, P]), id_f[:])
+        mr = kept("mr", [P, 2 * H], F32)
+        nc.vector.tensor_copy(out=mr[:], in_=mr_ps[:, 0 : 2 * H])
+        cb = kept("cb", [P, H, 6], F32)
+        nc.vector.memset(cb[:], -INV_N)
+        mu_pair = mr[:, 0:H].unsqueeze(2).to_broadcast([P, H, 2])
+        r_pair = mr[:, H : 2 * H].unsqueeze(2).to_broadcast([P, H, 2])
+        sc = kept("sc", [P, NB], F32)
+        nc.vector.tensor_tensor(
+            out=sc[:].rearrange("p (h e) -> p h e", e=2),
+            in0=wb_ps[:, 0:NB].rearrange("p (h e) -> p h e", e=2),
+            in1=r_pair,
+            op=ALU.mult,
+        )
+        ca = kept("ca", [P, H], F32)
+        nc.vector.scalar_tensor_tensor(
+            out=ca[:], in0=mr[:, H : 2 * H], scalar=-INV_N, in1=mr[:, H : 2 * H], op0=ALU.mult, op1=ALU.mult
+        )
+        sc_mu = kept("sc_mu", [P, NB], F32)
+        nc.vector.tensor_tensor(
+            out=sc_mu[:].rearrange("p (h e) -> p h e", e=2),
+            in0=sc[:].rearrange("p (h e) -> p h e", e=2),
+            in1=mu_pair,
+            op=ALU.mult,
+        )
+        nc.vector.scalar_tensor_tensor(
+            out=cb[:, :, 4:6],
+            in0=ca[:].unsqueeze(2).to_broadcast([P, H, 2]),
+            scalar=-1.0,
+            in1=mu_pair,
+            op0=ALU.mult,
+            op1=ALU.mult,
+        )
+        sh = kept("sh", [P, NB], F32)
+        nc.vector.tensor_tensor(out=sh[:], in0=wb_ps[:, NB : 2 * NB], in1=sc_mu[:], op=ALU.subtract)
+
+        gf_codes = {(G, k): kept("gfc%d%d" % (G, k), [P, 512], U32) for G in range(2) for k in range(2)}
+        gf_scales = {(G, k): kept("gfs%d%d" % (G, k), [P, 512], U8) for G in range(2) for k in range(2)}
+        gt_codes = {(m, G): kept("gtc%d%d" % (m, G), [P, 256], U32) for m in range(4) for G in range(2)}
+        gt_scales = {(m, G): kept("gts%d%d" % (m, G), [P, 256], U8) for m in range(4) for G in range(2)}
+        h_codes, h_scales, w_codes, w_scales = {}, {}, {}, {}
+        xt_ps, h_t, h_grp, w_grp, gf_grp, gt_grp, dn, sums, coef, shift = {}, {}, {}, {}, {}, {}, {}, {}, {}, {}
+
+        def quantize(codes, scales, values, fmt):
+            nc.vector.quantize_mx(out=codes.bitcast(fmt), scales=scales, in_=values)
+
+        def transpose_x(b, tag):
+            c, cols = b // 4, slice((b % 4) * P, (b % 4 + 1) * P)
+            xt_ps[b] = bank(tag, [P, 2, 2, 2, P], BF16)
+            for G in range(2):
+                for u in range(2):
+                    for hf in range(2):
+                        nc.tensor.transpose(xt_ps[b][:, G, u, hf, :], x_sb[c, u][:, 2 * G + hf, cols], id_bf[:])
+
+        def make_h(b):
+            h_t[b] = ring("h_t", [P, S], BF16, 4)
+            nc.vector.tensor_scalar(
+                out=h_t[b][:],
+                in0=xt_ps[b][:].rearrange("p g u h q -> p (g u h q)"),
+                scalar1=sc[:, b : b + 1],
+                scalar2=sh[:, b : b + 1],
+                op0=ALU.mult,
+                op1=ALU.add,
+            )
+
+        def transpose_h(b, tag):
+            ps = bank(tag, [P, 2, 2, P], F32)
+            words = h_t[b][:].bitcast(F32)
+            for G in range(2):
+                for u in range(2):
+                    w0 = (2 * G + u) * P
+                    nc.tensor.transpose(ps[:, G, u, :], words[:, w0 : w0 + P], id_f[:])
+            h_grp[b] = ring("h_grp", [P, 2, 4 * P], BF16, 3)
+            nc.scalar.copy(
+                out=h_grp[b][:].bitcast(F32).rearrange("p g (c u) -> p g c u", u=2),
+                in_=ps[:].rearrange("p g u c -> p g c u"),
+            )
+
+        def quantize_h(b):
+            c, cols = b // 4, slice((b % 4) * P, (b % 4 + 1) * P)
+            for G in range(2):
+                if b % 4 == 0:
+                    h_codes[c, G] = ring("h_codes%d" % G, [P, CH], U32, 3)
+                    h_scales[c, G] = ring("h_scales%d" % G, [P, CH], U8, 3)
+                quantize(h_codes[c, G][:, cols], h_scales[c, G][:, cols], h_grp[b][:, G, :], E4)
+
+        def transpose_g(G, k, tags):
+            gf_grp[G, k] = ring("gf_grp", [P, 2, 1024], BF16, 2)
+            words = g_sb[G, k][:].bitcast(F32)
+            for u in range(2):
+                ps = bank(tags[u], [P, 4, P], F32)
+                for e in range(2):
+                    for w in range(2):
+                        nc.tensor.transpose(ps[:, 2 * e + w, :], words[:, 2 * e + u, w:256:2], id_f[:])
+                nc.scalar.copy(
+                    out=gf_grp[G, k][:, u, :].bitcast(F32).rearrange("p (t m) -> p t m", m=4),
+                    in_=ps[:].rearrange("p m t -> p t m"),
+                )
+
+        def quantize_gf(G, k):
+            quantize(gf_codes[G, k][:], gf_scales[G, k][:], gf_grp[G, k][:].rearrange("p u n -> p (u n)"), E5)
+
+        def move_on_gpsimd(out, in_):
+            nc.gpsimd.tensor_scalar(out=out, in0=in_, scalar1=1.0, scalar2=0.0, op0=ALU.mult, op1=ALU.add)
+
+        def move_on_scalar(out, in_):
+            nc.scalar.copy(out=out, in_=in_)
+
+        def interleave_g(m, G, move):
+            gt_grp[m, G] = ring("gt_grp", [P, 1024], BF16, 3)
+            src = g_sb[G, m // 2][:, :, (m % 2) * 256 : (m % 2 + 1) * 256]
+            move(
+                gt_grp[m, G][:].rearrange("p (d u e) -> p d u e", u=2, e=2),
+                src.rearrange("p (e u) d -> p d u e", u=2),
+            )
+
+        def quantize_gt(m, G):
+            quantize(gt_codes[m, G][:], gt_scales[m, G][:], gt_grp[m, G][:], E5)
+
+        def interleave_w(b):
+            c, cols = b // 4, slice((b % 4) * P, (b % 4 + 1) * P)
+            w_grp[b] = ring("w_grp", [P, 1024], BF16, 1)
+            move_on_gpsimd(
+                w_grp[b][:].rearrange("p (k c j) -> p k c j", k=2, j=4),
+                w_sb[c][:, :, :, cols].rearrange("p k j c -> p k c j"),
+            )
+
+        def quantize_w(b):
+            w_codes[b] = ring("w_codes", [P, 2 * P], U32, 3)
+            w_scales[b] = ring("w_scales", [P, 2 * P], U8, 3)
+            quantize(w_codes[b][:], w_scales[b][:], w_grp[b][:], E4)
+
+        def product_dh(b):
+            gam, e = b // 2, b % 2
+            if e == 0:
+                sums[gam] = ring("sums", [P, 8], F32, 2)
+            dn[b] = ring("dn", [P, S], F32, 6)
+            for G in range(2):
+                ps = bank("dh%d" % G, [P, 512], F32)
+                for k in range(2):
+                    nc.tensor.matmul_mx(
+                        out=ps[:],
+                        lhsT=w_codes[b][:, k * P : (k + 1) * P].bitcast(E4),
+                        lhsT_scale=w_scales[b][:, k * P : (k + 1) * P],
+                        rhs=gf_codes[G, k][:].bitcast(E5),
+                        rhs_scale=gf_scales[G, k][:],
+                        start=(k == 0),
+                        stop=(k == 1),
+                    )
+                nc.scalar.activation(
+                    out=dn[b][:, G * 512 : (G + 1) * 512],
+                    in_=ps[:],
+                    func=IDENT,
+                    scale=sc[:, b : b + 1],
+                    accum_out=sums[gam][:, 2 * e + G : 2 * e + G + 1],
+                )
+
+        def product_dw(c, m):
+            stage = ring("dw_stage", [P, 2, CH], F32, 4)
+            for t in range(2):
+                ps = bank("dw%d" % t, [P, CH], F32)
+                for G in range(2):
+                    nc.tensor.matmul_mx(
+                        out=ps[:],
+                        lhsT=gt_codes[m, G][:, t * P : (t + 1) * P].bitcast(E5),
+                        lhsT_scale=gt_scales[m, G][:, t * P : (t + 1) * P],
+                        rhs=h_codes[c, G][:].bitcast(E4),
+                        rhs_scale=h_scales[c, G][:],
+                        start=(G == 0),
+                        stop=(G == 1),
+                    )
+                nc.scalar.copy(out=stage[:, t, :], in_=ps[:])
+            nc.sync.dma_start(
+                out=out_1[256 * m : 256 * (m + 1), c * CH : (c + 1) * CH].rearrange("(t p) c -> p t c", p=P),
+                in_=stage[:],
+            )
+
+        def sum_dn_x(b):
+            gam, e = b // 2, b % 2
+            prod = ring("prod", [P, S], F32, 2)
+            nc.vector.scalar_tensor_tensor(
+                out=prod[:],
+                in0=xt_ps[b][:].rearrange("p g u h q -> p (g u h q)"),
+                scalar=mr[:, gam : gam + 1],
+                in1=dn[b][:],
+                op0=ALU.subtract,
+                op1=ALU.mult,
+                accum_out=sums[gam][:, 4 + e : 5 + e],
+            )
+
+        def group_coefficients(gam):
+            ps = bank("o1", [P, 6], F32)
+            nc.tensor.matmul(out=ps[:], lhsT=ones[:], rhs=sums[gam][:, 0:6], start=True, stop=True)
+            coef[gam] = ring("coef", [P, 2], F32, 3)
+            terms = ring("terms", [P, 8], F32, 2)
+            nc.vector.tensor_scalar(
+                out=terms[:, 0:2],
+                in0=ps[:, 4:6],
+                scalar1=ca[:, gam : gam + 1],
+                scalar2=None,
+                op0=ALU.mult,
+                op1=ALU.add,
+                accum_out=coef[gam][:, 0:1],
+            )
+            nc.vector.scalar_tensor_tensor(
+                out=terms[:, 2:8],
+                in0=ps[:],
+                scalar=1.0,
+                in1=cb[:, gam, :],
+                op0=ALU.mult,
+                op1=ALU.mult,
+                accum_out=coef[gam][:, 1:2],
+            )
+
+        def make_shift(gam, G, on_scalar):
+            c, cols = gam // 2, slice((gam % 2) * DH, (gam % 2 + 1) * DH)
+            for u in range(2):
+                shift[gam, G, u] = ring("shift", [P, 2, DH], F32, 4)
+                src = x_sb[c, u][:, 2 * G : 2 * G + 2, cols]
+                if on_scalar:
+                    nc.scalar.activation(
+                        out=shift[gam, G, u][:], in_=src, func=IDENT, scale=coef[gam][:, 0:1], bias=coef[gam][:, 1:2]
+                    )
+                else:
+                    nc.gpsimd.tensor_scalar(
+                        out=shift[gam, G, u][:],
+                        in0=src,
+                        scalar1=coef[gam][:, 0:1],
+                        scalar2=coef[gam][:, 1:2],
+                        op0=ALU.mult,
+                        op1=ALU.add,
+                    )
+
+        def finish_dx(gam, G, tags):
+            for u in range(2):
+                ps = bank(tags[u], [P, 2, DH], F32)
+                for hf in range(2):
+                    t0 = G * 512 + u * 256 + hf * P
+                    for e in range(2):
+                        nc.tensor.transpose(ps[:, hf, e * P : (e + 1) * P], dn[2 * gam + e][:, t0 : t0 + P], id_f[:])
+                stage = ring("dx_stage", [P, 2, DH], F32, 6)
+                nc.vector.tensor_tensor(out=stage[:], in0=ps[:], in1=shift[gam, G, u][:], op=ALU.add)
+                nc.sync.dma_start(out=oa[:, u, 2 * G : 2 * G + 2, gam * DH : (gam + 1) * DH], in_=stage[:])
+
+        for b in range(12, 16):
+            transpose_x(b, BANKS[b - 12])
+            make_h(b)
+        transpose_g(0, 0, ("xt", "hw"))
+        interleave_g(0, 0, move_on_gpsimd)
+        transpose_h(12, "o0")
+        transpose_h(13, "o1")
+        quantize_gf(0, 0)
+        quantize_h(12)
+        quantize_h(13)
+        transpose_g(0, 1, ("dh0", "dh1"))
+        interleave_g(1, 0, move_on_gpsimd)
+        transpose_h(14, "dw0")
+        transpose_h(15, "dw1")
+        quantize_gt(0, 0)
+        quantize_gf(0, 1)
+        quantize_h(14)
+        quantize_h(15)
+        interleave_w(0)
+        quantize_gt(1, 0)
+        quantize_w(0)
+        transpose_g(1, 0, ("xt", "hw"))
+        interleave_w(1)
+        transpose_g(1, 1, ("o0", "o1"))
+        quantize_gf(1, 0)
+        quantize_gf(1, 1)
+        quantize_w(1)
+
+        g_on_gpsimd = {0: (0, 1), 1: (1, 1)}
+        g_on_scalar = {0: (2, 0), 1: (3, 0), 2: (2, 1), 3: (3, 1)}
+
+        for i in range(NB + 2):
+            if i < NB:
+                product_dh(i)
+            if i >= DW_FIRST:
+                product_dw(DW_ORDER[(i - DW_FIRST) // 4], (i - DW_FIRST) % 4)
+            if i >= 2 and i % 2 == 0:
+                group_coefficients(i // 2 - 1)
+            if i < NB:
+                transpose_x(i, "xt")
+                if i < 12:
+                    make_h(i)
+                sum_dn_x(i)
+            if 1 <= i <= 12:
+                transpose_h(i - 1, "hw")
+            if i in g_on_scalar:
+                interleave_g(*g_on_scalar[i], move_on_scalar)
+            if i >= 3:
+                finish_dx((i - 3) // 2, (i - 3) % 2, ("o0", "o1"))
+            if i == NB + 1:
+                finish_dx(H - 1, 1, ("xt", "hw"))
+            if i + 2 < NB:
+                interleave_w(i + 2)
+            if i in g_on_gpsimd:
+                interleave_g(*g_on_gpsimd[i], move_on_gpsimd)
+            if 2 <= i <= NB:
+                make_shift((i - 2) // 2, i % 2, False)
+            if i == NB:
+                make_shift(H - 1, 1, True)
+            if 1 <= i <= 12:
+                quantize_h(i - 1)
+            if i in g_on_scalar:
+                quantize_gt(*g_on_scalar[i])
+            if i in g_on_gpsimd:
+                quantize_gt(*g_on_gpsimd[i])
+            if i + 2 < NB:
+                quantize_w(i + 2)

@@ -23,8 +23,7 @@ CH = 512
 NC = DI // CH
 INV_N = 1.0 / (S * DH)
 BANKS = ["dh0", "dh1", "dw0", "dw1", "xt", "hw", "o0", "o1"]
-DW_ORDER = [3, 0, 1, 2]
-DW_FIRST = 2
+H_ON_SCALAR = 512
 
 
 def tile_mlstmblock_pb_v_kernel(
@@ -62,77 +61,89 @@ def tile_mlstmblock_pb_v_kernel(
         ones = kept("ones", [P, P], F32)
         nc.scalar.activation(out=ones[:], in_=id_bf[:], func=IDENT, scale=0.0, bias=1.0)
 
-        nc.sync.dma_start(out=wb_rows[0:NB, :], in_=gn_w.rearrange("(b p) -> b p", p=P))
-        nc.sync.dma_start(out=wb_rows[NB : 2 * NB, :], in_=gn_b.rearrange("(b p) -> b p", p=P))
-        with nc.allow_non_contiguous_dma(reason="one float32 value to a partition"):
-            nc.sync.dma_start(out=mr_col[0:H, 0:1], in_=mu.rearrange("b h -> h b"))
-            nc.sync.dma_start(out=mr_col[H : 2 * H, 0:1], in_=rstd.rearrange("b h -> h b"))
-
         x_sb, w_sb, g_sb = {}, {}, {}
 
-        def load_x(c):
+        def load_x(g0, n):
             for u in range(2):
-                x_sb[c, u] = kept("x%d%d" % (c, u), [P, 4, CH], BF16)
-                nc.sync.dma_start(out=x_sb[c, u][:], in_=xa[:, u, :, c * CH : (c + 1) * CH])
+                t = kept("x%d%d" % (g0, u), [P, 4, n * DH], BF16)
+                nc.sync.dma_start(out=t[:], in_=xa[:, u, :, g0 * DH : (g0 + n) * DH])
+                for j in range(n):
+                    x_sb[g0 + j, u] = t[:, :, j * DH : (j + 1) * DH]
 
-        def load_w(c):
-            w_sb[c] = kept("w%d" % c, [P, 2, 4, CH], BF16)
+        def load_w(g0, n):
+            t = kept("w%d" % g0, [P, 2, 4, n * DH], BF16)
             for k in range(2):
-                nc.sync.dma_start(out=w_sb[c][:, k, :, :], in_=wa[:, k, :, c * CH : (c + 1) * CH])
+                nc.sync.dma_start(out=t[:, k, :, :], in_=wa[:, k, :, g0 * DH : (g0 + n) * DH])
+            for j in range(n):
+                w_sb[g0 + j] = t[:, :, :, j * DH : (j + 1) * DH]
 
         def load_g(G):
             for k in range(2):
                 g_sb[G, k] = kept("g%d%d" % (G, k), [P, 4, 512], BF16)
                 nc.sync.dma_start(out=g_sb[G, k][:], in_=ga[:, G, :, k * 512 : (k + 1) * 512])
 
-        load_x(3)
         load_g(0)
-        load_w(0)
+        nc.sync.dma_start(out=wb_rows[0:NB, :], in_=gn_w.rearrange("(b p) -> b p", p=P))
+        nc.sync.dma_start(out=wb_rows[NB : 2 * NB, :], in_=gn_b.rearrange("(b p) -> b p", p=P))
+        with nc.allow_non_contiguous_dma(reason="one float32 value to a partition"):
+            nc.sync.dma_start(out=mr_col[0:H, 0:1], in_=mu.rearrange("b h -> h b"))
+            nc.sync.dma_start(out=mr_col[H : 2 * H, 0:1], in_=rstd.rearrange("b h -> h b"))
         load_g(1)
-        load_x(0)
-        for c in range(1, 3):
-            load_w(c)
-            load_x(c)
-        load_w(3)
+        load_w(0, 1)
+        load_x(0, 1)
+        load_w(1, 1)
+        load_x(1, 1)
+        load_w(2, 2)
+        load_x(2, 2)
 
-        wb_ps = bank("o0", [P, P], BF16)
-        nc.tensor.transpose(wb_ps[:], wb_rows[:], id_bf[:])
-        mr_ps = bank("o1", [P, P], F32)
-        nc.tensor.transpose(mr_ps[:], mr_col[:, 0:1].to_broadcast([P, P]), id_f[:])
         mr = kept("mr", [P, 2 * H], F32)
-        nc.vector.tensor_copy(out=mr[:], in_=mr_ps[:, 0 : 2 * H])
-        cb = kept("cb", [P, H, 6], F32)
+        cb = kept("cb", [P, H, 8], F32)
+        sc = kept("sc", [P, NB], F32)
+        ca = kept("ca", [P, H], F32)
+        sc_mu = kept("sc_mu", [P, NB], F32)
+        sh = kept("sh", [P, NB], F32)
         nc.vector.memset(cb[:], -INV_N)
+
         mu_pair = mr[:, 0:H].unsqueeze(2).to_broadcast([P, H, 2])
         r_pair = mr[:, H : 2 * H].unsqueeze(2).to_broadcast([P, H, 2])
-        sc = kept("sc", [P, NB], F32)
-        nc.vector.tensor_tensor(
-            out=sc[:].rearrange("p (h e) -> p h e", e=2),
-            in0=wb_ps[:, 0:NB].rearrange("p (h e) -> p h e", e=2),
-            in1=r_pair,
-            op=ALU.mult,
-        )
-        ca = kept("ca", [P, H], F32)
-        nc.vector.scalar_tensor_tensor(
-            out=ca[:], in0=mr[:, H : 2 * H], scalar=-INV_N, in1=mr[:, H : 2 * H], op0=ALU.mult, op1=ALU.mult
-        )
-        sc_mu = kept("sc_mu", [P, NB], F32)
-        nc.vector.tensor_tensor(
-            out=sc_mu[:].rearrange("p (h e) -> p h e", e=2),
-            in0=sc[:].rearrange("p (h e) -> p h e", e=2),
-            in1=mu_pair,
-            op=ALU.mult,
-        )
-        nc.vector.scalar_tensor_tensor(
-            out=cb[:, :, 4:6],
-            in0=ca[:].unsqueeze(2).to_broadcast([P, H, 2]),
-            scalar=-1.0,
-            in1=mu_pair,
-            op0=ALU.mult,
-            op1=ALU.mult,
-        )
-        sh = kept("sh", [P, NB], F32)
-        nc.vector.tensor_tensor(out=sh[:], in0=wb_ps[:, NB : 2 * NB], in1=sc_mu[:], op=ALU.subtract)
+        wb_ps = {}
+
+        def constants_0():
+            wb_ps[0] = bank("xt", [P, P], BF16)
+            nc.tensor.transpose(wb_ps[0][:], wb_rows[:], id_bf[:])
+            mr_ps = bank("hw", [P, P], F32)
+            nc.tensor.transpose(mr_ps[:], mr_col[:, 0:1].to_broadcast([P, P]), id_f[:])
+            nc.vector.tensor_copy(out=mr[:], in_=mr_ps[:, 0 : 2 * H])
+
+        def constants_1():
+            nc.vector.tensor_tensor(
+                out=sc[:].rearrange("p (h e) -> p h e", e=2),
+                in0=wb_ps[0][:, 0:NB].rearrange("p (h e) -> p h e", e=2),
+                in1=r_pair,
+                op=ALU.mult,
+            )
+            nc.vector.scalar_tensor_tensor(
+                out=ca[:], in0=mr[:, H : 2 * H], scalar=-INV_N, in1=mr[:, H : 2 * H], op0=ALU.mult, op1=ALU.mult
+            )
+
+        def constants_2():
+            nc.vector.tensor_tensor(
+                out=sc_mu[:].rearrange("p (h e) -> p h e", e=2),
+                in0=sc[:].rearrange("p (h e) -> p h e", e=2),
+                in1=mu_pair,
+                op=ALU.mult,
+            )
+            nc.vector.scalar_tensor_tensor(
+                out=cb[:, :, 4:8],
+                in0=ca[:].unsqueeze(2).to_broadcast([P, H, 4]),
+                scalar=-1.0,
+                in1=mr[:, 0:H].unsqueeze(2).to_broadcast([P, H, 4]),
+                op0=ALU.mult,
+                op1=ALU.mult,
+            )
+
+        def constants_3():
+            nc.vector.tensor_tensor(out=sh[:], in0=wb_ps[0][:, NB : 2 * NB], in1=sc_mu[:], op=ALU.subtract)
 
         gf_codes = {(G, k): kept("gfc%d%d" % (G, k), [P, 512], U32) for G in range(2) for k in range(2)}
         gf_scales = {(G, k): kept("gfs%d%d" % (G, k), [P, 512], U8) for G in range(2) for k in range(2)}
@@ -141,27 +152,46 @@ def tile_mlstmblock_pb_v_kernel(
         h_codes, h_scales, w_codes, w_scales = {}, {}, {}, {}
         xt_ps, h_t, h_grp, w_grp, gf_grp, gt_grp, dn, sums, coef, shift = {}, {}, {}, {}, {}, {}, {}, {}, {}, {}
 
+        tot_ps, dx_ps = {}, {}
+
         def quantize(codes, scales, values, fmt):
             nc.vector.quantize_mx(out=codes.bitcast(fmt), scales=scales, in_=values)
 
-        def transpose_x(b, tag):
-            c, cols = b // 4, slice((b % 4) * P, (b % 4 + 1) * P)
+        def transpose_x(b, tag, plain=False):
+            cols = slice((b % 2) * P, (b % 2 + 1) * P)
             xt_ps[b] = bank(tag, [P, 2, 2, 2, P], BF16)
             for G in range(2):
                 for u in range(2):
                     for hf in range(2):
-                        nc.tensor.transpose(xt_ps[b][:, G, u, hf, :], x_sb[c, u][:, 2 * G + hf, cols], id_bf[:])
+                        nc.tensor.matmul(
+                            out=xt_ps[b][:, G, u, hf, :],
+                            lhsT=x_sb[b // 2, u][:, 2 * G + hf, cols],
+                            rhs=id_bf[:],
+                            start=True,
+                            stop=True,
+                            is_transpose=not plain,
+                        )
 
-        def make_h(b):
+        def make_h(b, n_scalar):
             h_t[b] = ring("h_t", [P, S], BF16, 4)
-            nc.vector.tensor_scalar(
-                out=h_t[b][:],
-                in0=xt_ps[b][:].rearrange("p g u h q -> p (g u h q)"),
-                scalar1=sc[:, b : b + 1],
-                scalar2=sh[:, b : b + 1],
-                op0=ALU.mult,
-                op1=ALU.add,
-            )
+            src = xt_ps[b][:].rearrange("p g u h q -> p (g u h q)")
+            if n_scalar:
+                nc.scalar.activation(
+                    out=h_t[b][:, 0:n_scalar],
+                    in_=src[:, 0:n_scalar],
+                    func=IDENT,
+                    scale=sc[:, b : b + 1],
+                    bias=sh[:, b : b + 1],
+                )
+            if n_scalar < S:
+                nc.vector.tensor_scalar(
+                    out=h_t[b][:, n_scalar:S],
+                    in0=src[:, n_scalar:S],
+                    scalar1=sc[:, b : b + 1],
+                    scalar2=sh[:, b : b + 1],
+                    op0=ALU.mult,
+                    op1=ALU.add,
+                )
 
         def transpose_h(b, tag):
             ps = bank(tag, [P, 2, 2, P], F32)
@@ -177,9 +207,10 @@ def tile_mlstmblock_pb_v_kernel(
             )
 
         def quantize_h(b):
-            c, cols = b // 4, slice((b % 4) * P, (b % 4 + 1) * P)
+            c, slot = divmod(b, 4)
+            cols = slice(slot * P, (slot + 1) * P)
             for G in range(2):
-                if b % 4 == 0:
+                if slot == 0:
                     h_codes[c, G] = ring("h_codes%d" % G, [P, CH], U32, 3)
                     h_scales[c, G] = ring("h_scales%d" % G, [P, CH], U8, 3)
                 quantize(h_codes[c, G][:, cols], h_scales[c, G][:, cols], h_grp[b][:, G, :], E4)
@@ -203,62 +234,72 @@ def tile_mlstmblock_pb_v_kernel(
         def move_on_gpsimd(out, in_):
             nc.gpsimd.tensor_scalar(out=out, in0=in_, scalar1=1.0, scalar2=0.0, op0=ALU.mult, op1=ALU.add)
 
+        def move_on_vector(out, in_):
+            nc.vector.tensor_copy(out=out, in_=in_)
+
         def move_on_scalar(out, in_):
             nc.scalar.copy(out=out, in_=in_)
 
         def interleave_g(m, G, move):
-            gt_grp[m, G] = ring("gt_grp", [P, 1024], BF16, 3)
+            gt_grp[m, G] = ring("gt_grp", [P, 1024], BF16, 4)
             src = g_sb[G, m // 2][:, :, (m % 2) * 256 : (m % 2 + 1) * 256]
             move(
-                gt_grp[m, G][:].rearrange("p (d u e) -> p d u e", u=2, e=2),
-                src.rearrange("p (e u) d -> p d u e", u=2),
+                gt_grp[m, G][:].rearrange("p (d i u e) -> p d u e i", i=4, u=2, e=2),
+                src.rearrange("p (e u) (d i) -> p d u e i", u=2, i=4),
             )
 
         def quantize_gt(m, G):
             quantize(gt_codes[m, G][:], gt_scales[m, G][:], gt_grp[m, G][:], E5)
 
-        def interleave_w(b):
-            c, cols = b // 4, slice((b % 4) * P, (b % 4 + 1) * P)
+        def interleave_w(b, on_vector):
+            cols = slice((b % 2) * P, (b % 2 + 1) * P)
             w_grp[b] = ring("w_grp", [P, 1024], BF16, 1)
-            move_on_gpsimd(
-                w_grp[b][:].rearrange("p (k c j) -> p k c j", k=2, j=4),
-                w_sb[c][:, :, :, cols].rearrange("p k j c -> p k c j"),
-            )
+            src = w_sb[b // 2][:, :, :, cols]
+            if on_vector:
+                move_on_vector(
+                    w_grp[b][:].rearrange("p (k c i j) -> p k c j i", k=2, i=4, j=4),
+                    src.rearrange("p k j (c i) -> p k c j i", i=4),
+                )
+            else:
+                move_on_gpsimd(
+                    w_grp[b][:].rearrange("p (k c j) -> p k c j", k=2, j=4), src.rearrange("p k j c -> p k c j")
+                )
 
         def quantize_w(b):
             w_codes[b] = ring("w_codes", [P, 2 * P], U32, 3)
             w_scales[b] = ring("w_scales", [P, 2 * P], U8, 3)
             quantize(w_codes[b][:], w_scales[b][:], w_grp[b][:], E4)
 
-        def product_dh(b):
+        def product_dh(b, G):
             gam, e = b // 2, b % 2
-            if e == 0:
-                sums[gam] = ring("sums", [P, 8], F32, 2)
-            dn[b] = ring("dn", [P, S], F32, 6)
-            for G in range(2):
-                ps = bank("dh%d" % G, [P, 512], F32)
-                for k in range(2):
-                    nc.tensor.matmul_mx(
-                        out=ps[:],
-                        lhsT=w_codes[b][:, k * P : (k + 1) * P].bitcast(E4),
-                        lhsT_scale=w_scales[b][:, k * P : (k + 1) * P],
-                        rhs=gf_codes[G, k][:].bitcast(E5),
-                        rhs_scale=gf_scales[G, k][:],
-                        start=(k == 0),
-                        stop=(k == 1),
-                    )
-                nc.scalar.activation(
-                    out=dn[b][:, G * 512 : (G + 1) * 512],
-                    in_=ps[:],
-                    func=IDENT,
-                    scale=sc[:, b : b + 1],
-                    accum_out=sums[gam][:, 2 * e + G : 2 * e + G + 1],
+            if G == 0:
+                if e == 0:
+                    sums[gam] = ring("sums", [P, 8], F32, 2)
+                dn[b] = ring("dn", [P, S], F32, 6)
+            ps = bank("dh%d" % G, [P, 512], F32)
+            for k in range(2):
+                nc.tensor.matmul_mx(
+                    out=ps[:],
+                    lhsT=w_codes[b][:, k * P : (k + 1) * P].bitcast(E4),
+                    lhsT_scale=w_scales[b][:, k * P : (k + 1) * P],
+                    rhs=gf_codes[G, k][:].bitcast(E5),
+                    rhs_scale=gf_scales[G, k][:],
+                    start=(k == 0),
+                    stop=(k == 1),
                 )
+            nc.scalar.activation(
+                out=dn[b][:, G * 512 : (G + 1) * 512],
+                in_=ps[:],
+                func=IDENT,
+                scale=sc[:, b : b + 1],
+                accum_out=sums[gam][:, 2 * e + G : 2 * e + G + 1],
+            )
 
-        def product_dw(c, m):
+        def product_dw(c, m, tags, moves, split=False):
             stage = ring("dw_stage", [P, 2, CH], F32, 4)
+            rows = out_1[256 * m : 256 * (m + 1), c * CH : (c + 1) * CH].rearrange("(t p) c -> p t c", p=P)
             for t in range(2):
-                ps = bank("dw%d" % t, [P, CH], F32)
+                ps = bank(tags[t], [P, CH], F32)
                 for G in range(2):
                     nc.tensor.matmul_mx(
                         out=ps[:],
@@ -269,33 +310,36 @@ def tile_mlstmblock_pb_v_kernel(
                         start=(G == 0),
                         stop=(G == 1),
                     )
-                nc.scalar.copy(out=stage[:, t, :], in_=ps[:])
-            nc.sync.dma_start(
-                out=out_1[256 * m : 256 * (m + 1), c * CH : (c + 1) * CH].rearrange("(t p) c -> p t c", p=P),
-                in_=stage[:],
-            )
+                moves[t](stage[:, t, :], ps[:])
+                if split:
+                    nc.sync.dma_start(out=rows[:, t, :], in_=stage[:, t, :])
+            if not split:
+                nc.sync.dma_start(out=rows, in_=stage[:])
 
-        def sum_dn_x(b):
+        def sum_dn_x(b, G):
             gam, e = b // 2, b % 2
-            prod = ring("prod", [P, S], F32, 2)
+            prod = ring("prod", [P, 512], F32, 2)
+            col = 4 + 2 * e + G
             nc.vector.scalar_tensor_tensor(
                 out=prod[:],
-                in0=xt_ps[b][:].rearrange("p g u h q -> p (g u h q)"),
+                in0=xt_ps[b][:, G, :, :, :].rearrange("p u h q -> p (u h q)"),
                 scalar=mr[:, gam : gam + 1],
-                in1=dn[b][:],
+                in1=dn[b][:, G * 512 : (G + 1) * 512],
                 op0=ALU.subtract,
                 op1=ALU.mult,
-                accum_out=sums[gam][:, 4 + e : 5 + e],
+                accum_out=sums[gam][:, col : col + 1],
             )
 
-        def group_coefficients(gam):
-            ps = bank("o1", [P, 6], F32)
-            nc.tensor.matmul(out=ps[:], lhsT=ones[:], rhs=sums[gam][:, 0:6], start=True, stop=True)
+        def group_sums(gam, tag, n):
+            tot_ps[gam] = bank(tag, [P, n], F32)
+            nc.tensor.matmul(out=tot_ps[gam][:], lhsT=ones[:], rhs=sums[gam][:, 0:n], start=True, stop=True)
+
+        def group_coefficients(gam, n):
             coef[gam] = ring("coef", [P, 2], F32, 3)
-            terms = ring("terms", [P, 8], F32, 2)
+            terms = ring("terms", [P, 16], F32, 2)
             nc.vector.tensor_scalar(
-                out=terms[:, 0:2],
-                in0=ps[:, 4:6],
+                out=terms[:, 0 : n - 4],
+                in0=tot_ps[gam][:, 4:n],
                 scalar1=ca[:, gam : gam + 1],
                 scalar2=None,
                 op0=ALU.mult,
@@ -303,109 +347,139 @@ def tile_mlstmblock_pb_v_kernel(
                 accum_out=coef[gam][:, 0:1],
             )
             nc.vector.scalar_tensor_tensor(
-                out=terms[:, 2:8],
-                in0=ps[:],
+                out=terms[:, 8 : 8 + n],
+                in0=tot_ps[gam][:],
                 scalar=1.0,
-                in1=cb[:, gam, :],
+                in1=cb[:, gam, 0:n],
                 op0=ALU.mult,
                 op1=ALU.mult,
                 accum_out=coef[gam][:, 1:2],
             )
 
-        def make_shift(gam, G, on_scalar):
-            c, cols = gam // 2, slice((gam % 2) * DH, (gam % 2 + 1) * DH)
-            for u in range(2):
-                shift[gam, G, u] = ring("shift", [P, 2, DH], F32, 4)
-                src = x_sb[c, u][:, 2 * G : 2 * G + 2, cols]
-                if on_scalar:
-                    nc.scalar.activation(
-                        out=shift[gam, G, u][:], in_=src, func=IDENT, scale=coef[gam][:, 0:1], bias=coef[gam][:, 1:2]
-                    )
-                else:
-                    nc.gpsimd.tensor_scalar(
-                        out=shift[gam, G, u][:],
-                        in0=src,
-                        scalar1=coef[gam][:, 0:1],
-                        scalar2=coef[gam][:, 1:2],
-                        op0=ALU.mult,
-                        op1=ALU.add,
+        def make_shift(gam, G, u, on_scalar):
+            shift[gam, G, u] = ring("shift", [P, 2, DH], F32, 6)
+            src = x_sb[gam, u][:, 2 * G : 2 * G + 2, :]
+            if on_scalar:
+                nc.scalar.activation(
+                    out=shift[gam, G, u][:], in_=src, func=IDENT, scale=coef[gam][:, 0:1], bias=coef[gam][:, 1:2]
+                )
+            else:
+                nc.gpsimd.tensor_scalar(
+                    out=shift[gam, G, u][:],
+                    in0=src,
+                    scalar1=coef[gam][:, 0:1],
+                    scalar2=coef[gam][:, 1:2],
+                    op0=ALU.mult,
+                    op1=ALU.add,
+                )
+
+        def transpose_dn(gam, G, u, tag):
+            dx_ps[gam, G, u] = bank(tag, [P, 2, DH], F32)
+            for hf in range(2):
+                t0 = G * 512 + u * 256 + hf * P
+                for e in range(2):
+                    nc.tensor.transpose(
+                        dx_ps[gam, G, u][:, hf, e * P : (e + 1) * P], dn[2 * gam + e][:, t0 : t0 + P], id_f[:]
                     )
 
-        def finish_dx(gam, G, tags):
-            for u in range(2):
-                ps = bank(tags[u], [P, 2, DH], F32)
-                for hf in range(2):
-                    t0 = G * 512 + u * 256 + hf * P
-                    for e in range(2):
-                        nc.tensor.transpose(ps[:, hf, e * P : (e + 1) * P], dn[2 * gam + e][:, t0 : t0 + P], id_f[:])
-                stage = ring("dx_stage", [P, 2, DH], F32, 6)
-                nc.vector.tensor_tensor(out=stage[:], in0=ps[:], in1=shift[gam, G, u][:], op=ALU.add)
-                nc.sync.dma_start(out=oa[:, u, 2 * G : 2 * G + 2, gam * DH : (gam + 1) * DH], in_=stage[:])
+        def finish_dx(gam, G, u):
+            stage = ring("dx_stage", [P, 2, DH], F32, 6)
+            nc.vector.tensor_tensor(out=stage[:], in0=dx_ps[gam, G, u][:], in1=shift[gam, G, u][:], op=ALU.add)
+            nc.sync.dma_start(out=oa[:, u, 2 * G : 2 * G + 2, gam * DH : (gam + 1) * DH], in_=stage[:])
 
-        for b in range(12, 16):
-            transpose_x(b, BANKS[b - 12])
-            make_h(b)
-        transpose_g(0, 0, ("xt", "hw"))
-        interleave_g(0, 0, move_on_gpsimd)
-        transpose_h(12, "o0")
-        transpose_h(13, "o1")
-        quantize_gf(0, 0)
-        quantize_h(12)
-        quantize_h(13)
-        transpose_g(0, 1, ("dh0", "dh1"))
-        interleave_g(1, 0, move_on_gpsimd)
-        transpose_h(14, "dw0")
-        transpose_h(15, "dw1")
-        quantize_gt(0, 0)
-        quantize_gf(0, 1)
-        quantize_h(14)
-        quantize_h(15)
-        interleave_w(0)
+        interleave_g(0, 0, move_on_scalar)
+        interleave_g(1, 0, move_on_vector)
+        transpose_g(0, 0, ("o0", "o1"))
+        interleave_g(2, 0, move_on_scalar)
         quantize_gt(1, 0)
+        interleave_g(3, 0, move_on_vector)
+        quantize_gt(0, 0)
+        constants_0()
+        quantize_gt(3, 0)
+        constants_1()
+        transpose_g(0, 1, ("dw0", "dw1"))
+        quantize_gf(0, 0)
+        constants_2()
+        interleave_g(0, 1, move_on_vector)
+        constants_3()
+        quantize_gt(2, 0)
+        interleave_g(1, 1, move_on_vector)
+        quantize_gt(0, 1)
+        quantize_gf(0, 1)
+        transpose_g(1, 0, ("o0", "o1"))
+        interleave_w(0, True)
+        quantize_gt(1, 1)
         quantize_w(0)
-        transpose_g(1, 0, ("xt", "hw"))
-        interleave_w(1)
-        transpose_g(1, 1, ("o0", "o1"))
+        transpose_g(1, 1, ("xt", "hw"))
         quantize_gf(1, 0)
+        interleave_w(1, True)
+        product_dh(0, 0)
+        transpose_x(0, "dw0")
         quantize_gf(1, 1)
-        quantize_w(1)
 
-        g_on_gpsimd = {0: (0, 1), 1: (1, 1)}
-        g_on_scalar = {0: (2, 0), 1: (3, 0), 2: (2, 1), 3: (3, 1)}
+        DW0 = 4
+        late_loads = {1: (load_w, 4, 2), 2: (load_x, 4, 2), 3: (load_w, 6, 2), 4: (load_x, 6, 2)}
+        LAST = NB - 1
+        on_scalar = (move_on_scalar, move_on_scalar)
 
-        for i in range(NB + 2):
-            if i < NB:
-                product_dh(i)
-            if i >= DW_FIRST:
-                product_dw(DW_ORDER[(i - DW_FIRST) // 4], (i - DW_FIRST) % 4)
-            if i >= 2 and i % 2 == 0:
-                group_coefficients(i // 2 - 1)
-            if i < NB:
-                transpose_x(i, "xt")
-                if i < 12:
-                    make_h(i)
-                sum_dn_x(i)
-            if 1 <= i <= 12:
-                transpose_h(i - 1, "hw")
-            if i in g_on_scalar:
-                interleave_g(*g_on_scalar[i], move_on_scalar)
-            if i >= 3:
-                finish_dx((i - 3) // 2, (i - 3) % 2, ("o0", "o1"))
-            if i == NB + 1:
-                finish_dx(H - 1, 1, ("xt", "hw"))
-            if i + 2 < NB:
-                interleave_w(i + 2)
-            if i in g_on_gpsimd:
-                interleave_g(*g_on_gpsimd[i], move_on_gpsimd)
-            if 2 <= i <= NB:
-                make_shift((i - 2) // 2, i % 2, False)
-            if i == NB:
-                make_shift(H - 1, 1, True)
-            if 1 <= i <= 12:
+        for i in range(NB):
+            stats = i >= 2 and i % 2 == 0
+            early = i < DW0
+            if i in late_loads:
+                late_loads[i][0](*late_loads[i][1:])
+            if i >= 1:
                 quantize_h(i - 1)
-            if i in g_on_scalar:
-                quantize_gt(*g_on_scalar[i])
-            if i in g_on_gpsimd:
-                quantize_gt(*g_on_gpsimd[i])
+            if i < 2:
+                interleave_g(i + 2, 1, move_on_vector)
+            if i + 1 < NB:
+                quantize_w(i + 1)
+            if i < 2:
+                quantize_gt(i + 2, 1)
             if i + 2 < NB:
-                quantize_w(i + 2)
+                interleave_w(i + 2, False)
+            if i >= 3:
+                finish_dx((i - 3) // 2, (i - 3) % 2, 1)
+            make_h(i, S if early else H_ON_SCALAR)
+            if i > 0:
+                product_dh(i, 0)
+            product_dh(i, 1)
+            if stats:
+                group_sums(i // 2 - 1, "hw", 8)
+            if i == LAST:
+                transpose_h(i, "hw")
+            if not early:
+                product_dw((i - DW0) // 4, (i - DW0) % 4, ("dw0", "dw1"), on_scalar)
+            if stats:
+                group_coefficients(i // 2 - 1, 8)
+            sum_dn_x(i, 0)
+            if i >= 2:
+                for u in range(2):
+                    make_shift((i - 2) // 2, i % 2, u, False)
+            sum_dn_x(i, 1)
+            if early:
+                transpose_x(i + 1, "dw%d" % ((i + 1) % 2) if i + 1 < DW0 else "xt")
+            if i < LAST:
+                transpose_h(i, "hw")
+            else:
+                quantize_h(LAST)
+            if i >= 2:
+                for u in range(2):
+                    transpose_dn((i - 2) // 2, i % 2, u, "o%d" % u)
+                finish_dx((i - 2) // 2, i % 2, 0)
+            if not early and i < LAST:
+                transpose_x(i + 1, "xt")
+
+        gam = H - 1
+        group_sums(gam, "xt", 8)
+        group_coefficients(gam, 8)
+        finish_dx(gam - 1, 1, 1)
+        order = [(0, 0), (1, 0), (0, 1), (1, 1)]
+        for G, u in order:
+            make_shift(gam, G, u, False)
+        product_dw(3, 0, ("dh0", "dh1"), on_scalar)
+        product_dw(3, 1, ("dw0", "dw1"), on_scalar)
+        for n, (G, u) in enumerate(order):
+            transpose_dn(gam, G, u, ("hw", "o0", "xt", "o1")[n])
+            finish_dx(gam, G, u)
+        product_dw(3, 2, ("dh0", "dh1"), on_scalar)
+        product_dw(3, 3, ("dw0", "dw1"), on_scalar, split=True)

@@ -12,28 +12,27 @@ F32 = mybir.dt.float32
 BF16 = mybir.dt.bfloat16
 U32 = mybir.dt.uint32
 U8 = mybir.dt.uint8
-E4 = mybir.dt.float8_e4m3fn_x4
-E5 = mybir.dt.float8_e5m2_x4
+E4M3 = mybir.dt.float8_e4m3fn_x4
+E5M2 = mybir.dt.float8_e5m2_x4
 ALU = mybir.AluOpType
-IDENT = mybir.ActivationFunctionType.Identity
+IDENTITY = mybir.ActivationFunctionType.Identity
 
 P = 128
-NB = DI // P
-CH = 512
-NC = DI // CH
+HALF = 512
+CHUNK = 512
+STEPS = 2 * H
+DW_LAG = 4
 INV_N = 1.0 / (S * DH)
-BANKS = ["dh0", "dh1", "dw0", "dw1", "xt", "hw", "o0", "o1"]
-H_ON_SCALAR = 512
 
 
 def tile_mlstmblock_pb_v_kernel(
     tc, h_attn, gn_w, gn_b, W_out, x, skip_scale, mu, rstd, grad_out, out_0, out_1
 ):
     nc = tc.nc
-    xa = h_attn.rearrange("b (s q u) c -> q u (b s) c", q=P, u=2)
-    oa = out_0.rearrange("b (s q u) c -> q u (b s) c", q=P, u=2)
-    ga = grad_out.rearrange("b (g p j) d -> p (b g) j d", p=P, j=4)
-    wa = W_out.rearrange("(k p j) c -> p k j c", p=P, j=4)
+    ha_hbm = h_attn.rearrange("b (s q u) c -> q u (b s) c", q=P, u=2)
+    dx_hbm = out_0.rearrange("b (s q u) c -> q u (b s) c", q=P, u=2)
+    g_hbm = grad_out.rearrange("b (g p j) d -> p (b g) j d", p=P, j=4)
+    w_hbm = W_out.rearrange("(k p j) c -> p k j c", p=P, j=4)
 
     with ExitStack() as ctx:
         keep = ctx.enter_context(tc.tile_pool(name="keep", bufs=1))
@@ -50,436 +49,425 @@ def tile_mlstmblock_pb_v_kernel(
         def bank(tag, shape, dtype):
             return psum.tile(shape, dtype, name=tag, tag=tag)
 
-        wb_rows = kept("wb_rows", [P, P], BF16)
+        wb_rows = kept("wb_rows", [P, DH], BF16)
         mr_col = kept("mr_col", [P, 8], F32)
         nc.vector.memset(wb_rows[:], 0.0)
-        nc.vector.memset(mr_col[:], 0.0)
-        id_bf = kept("id_bf", [P, P], BF16)
-        id_f = kept("id_f", [P, P], F32)
-        make_identity(nc, id_bf[:])
-        make_identity(nc, id_f[:])
+        nc.vector.memset(mr_col[:, 0:1], 0.0)
+        ident = kept("ident", [P, P], F32)
+        make_identity(nc, ident[:])
         ones = kept("ones", [P, P], F32)
-        nc.scalar.activation(out=ones[:], in_=id_bf[:], func=IDENT, scale=0.0, bias=1.0)
+        nc.scalar.activation(out=ones[:], in_=ident[:], func=IDENTITY, scale=0.0, bias=1.0)
 
-        x_sb, w_sb, g_sb = {}, {}, {}
+        ha_sb, w_sb, g_sb = {}, {}, {}
 
-        def load_x(g0, n):
+        def load_ha(first, n):
             for u in range(2):
-                t = kept("x%d%d" % (g0, u), [P, 4, n * DH], BF16)
-                nc.sync.dma_start(out=t[:], in_=xa[:, u, :, g0 * DH : (g0 + n) * DH])
+                t = kept("ha%d_%d" % (first, u), [P, 4, n * DH], BF16)
+                nc.sync.dma_start(out=t[:], in_=ha_hbm[:, u, :, first * DH : (first + n) * DH])
                 for j in range(n):
-                    x_sb[g0 + j, u] = t[:, :, j * DH : (j + 1) * DH]
+                    ha_sb[first + j, u] = t[:, :, j * DH : (j + 1) * DH]
 
-        def load_w(g0, n):
-            t = kept("w%d" % g0, [P, 2, 4, n * DH], BF16)
+        def load_w(first, n):
+            t = kept("w%d" % first, [P, 2, 4, n * DH], BF16)
             for k in range(2):
-                nc.sync.dma_start(out=t[:, k, :, :], in_=wa[:, k, :, g0 * DH : (g0 + n) * DH])
+                nc.sync.dma_start(out=t[:, k, :, :], in_=w_hbm[:, k, :, first * DH : (first + n) * DH])
             for j in range(n):
-                w_sb[g0 + j] = t[:, :, :, j * DH : (j + 1) * DH]
+                w_sb[first + j] = t[:, :, :, j * DH : (j + 1) * DH]
 
         def load_g(G):
             for k in range(2):
-                g_sb[G, k] = kept("g%d%d" % (G, k), [P, 4, 512], BF16)
-                nc.sync.dma_start(out=g_sb[G, k][:], in_=ga[:, G, :, k * 512 : (k + 1) * 512])
+                g_sb[G, k] = kept("g%d_%d" % (G, k), [P, 4, HALF], BF16)
+                nc.sync.dma_start(out=g_sb[G, k][:], in_=g_hbm[:, G, :, k * HALF : (k + 1) * HALF])
 
         load_g(0)
-        nc.sync.dma_start(out=wb_rows[0:NB, :], in_=gn_w.rearrange("(b p) -> b p", p=P))
-        nc.sync.dma_start(out=wb_rows[NB : 2 * NB, :], in_=gn_b.rearrange("(b p) -> b p", p=P))
+        nc.sync.dma_start(out=wb_rows[0:H, :], in_=gn_w.rearrange("(h c) -> h c", c=DH))
+        nc.sync.dma_start(out=wb_rows[H : 2 * H, :], in_=gn_b.rearrange("(h c) -> h c", c=DH))
         with nc.allow_non_contiguous_dma(reason="one float32 value to a partition"):
             nc.sync.dma_start(out=mr_col[0:H, 0:1], in_=mu.rearrange("b h -> h b"))
             nc.sync.dma_start(out=mr_col[H : 2 * H, 0:1], in_=rstd.rearrange("b h -> h b"))
         load_g(1)
         load_w(0, 1)
-        load_x(0, 1)
+        load_ha(0, 1)
         load_w(1, 1)
-        load_x(1, 1)
+        load_ha(1, 1)
         load_w(2, 2)
-        load_x(2, 2)
+        load_ha(2, 2)
+        load_w(4, 2)
+        load_ha(4, 2)
 
         mr = kept("mr", [P, 2 * H], F32)
-        cb = kept("cb", [P, H, 8], F32)
-        sc = kept("sc", [P, NB], F32)
-        ca = kept("ca", [P, H], F32)
-        sc_mu = kept("sc_mu", [P, NB], F32)
-        sh = kept("sh", [P, NB], F32)
-        nc.vector.memset(cb[:], -INV_N)
+        scale = kept("scale", [P, H, 2], F32)
+        scale_mu = kept("scale_mu", [P, H, 2], F32)
+        offset = kept("offset", [P, H, 2], F32)
+        a_weight = kept("a_weight", [P, H], F32)
+        b_weights = kept("b_weights", [P, H, 8], F32)
+        nc.vector.memset(b_weights[:], -INV_N)
+        wb_t = {}
 
-        mu_pair = mr[:, 0:H].unsqueeze(2).to_broadcast([P, H, 2])
-        r_pair = mr[:, H : 2 * H].unsqueeze(2).to_broadcast([P, H, 2])
-        wb_ps = {}
+        def by_group(cols, n):
+            return cols.unsqueeze(2).to_broadcast([P, H, n])
 
-        def constants_0():
-            wb_ps[0] = bank("xt", [P, P], BF16)
-            nc.tensor.transpose(wb_ps[0][:], wb_rows[:], id_bf[:])
+        def constants_spread():
+            ps = bank("ha", [P, P], F32)
+            nc.tensor.transpose(ps[:], wb_rows[:].bitcast(F32), ident[:])
+            pairs = ps[:].bitcast(BF16).rearrange("p (r e) -> p r e", e=2)
+            wb_t["w"], wb_t["b"] = pairs[:, 0:H, :], pairs[:, H : 2 * H, :]
             mr_ps = bank("hw", [P, P], F32)
-            nc.tensor.transpose(mr_ps[:], mr_col[:, 0:1].to_broadcast([P, P]), id_f[:])
+            nc.tensor.transpose(mr_ps[:], mr_col[:, 0:1].to_broadcast([P, P]), ident[:])
             nc.vector.tensor_copy(out=mr[:], in_=mr_ps[:, 0 : 2 * H])
 
-        def constants_1():
-            nc.vector.tensor_tensor(
-                out=sc[:].rearrange("p (h e) -> p h e", e=2),
-                in0=wb_ps[0][:, 0:NB].rearrange("p (h e) -> p h e", e=2),
-                in1=r_pair,
-                op=ALU.mult,
-            )
-            nc.vector.scalar_tensor_tensor(
-                out=ca[:], in0=mr[:, H : 2 * H], scalar=-INV_N, in1=mr[:, H : 2 * H], op0=ALU.mult, op1=ALU.mult
-            )
+        def constants_scale():
+            r = mr[:, H : 2 * H]
+            nc.vector.tensor_tensor(out=scale[:], in0=wb_t["w"], in1=by_group(r, 2), op=ALU.mult)
+            nc.vector.scalar_tensor_tensor(out=a_weight[:], in0=r, scalar=-INV_N, in1=r, op0=ALU.mult, op1=ALU.mult)
 
-        def constants_2():
-            nc.vector.tensor_tensor(
-                out=sc_mu[:].rearrange("p (h e) -> p h e", e=2),
-                in0=sc[:].rearrange("p (h e) -> p h e", e=2),
-                in1=mu_pair,
-                op=ALU.mult,
-            )
+        def constants_mu():
+            nc.vector.tensor_tensor(out=scale_mu[:], in0=scale[:], in1=by_group(mr[:, 0:H], 2), op=ALU.mult)
             nc.vector.scalar_tensor_tensor(
-                out=cb[:, :, 4:8],
-                in0=ca[:].unsqueeze(2).to_broadcast([P, H, 4]),
+                out=b_weights[:, :, 4:8],
+                in0=by_group(a_weight[:], 4),
                 scalar=-1.0,
-                in1=mr[:, 0:H].unsqueeze(2).to_broadcast([P, H, 4]),
+                in1=by_group(mr[:, 0:H], 4),
                 op0=ALU.mult,
                 op1=ALU.mult,
             )
 
-        def constants_3():
-            nc.vector.tensor_tensor(out=sh[:], in0=wb_ps[0][:, NB : 2 * NB], in1=sc_mu[:], op=ALU.subtract)
+        def constants_offset():
+            nc.vector.tensor_tensor(out=offset[:], in0=wb_t["b"], in1=scale_mu[:], op=ALU.subtract)
 
-        gf_codes = {(G, k): kept("gfc%d%d" % (G, k), [P, 512], U32) for G in range(2) for k in range(2)}
-        gf_scales = {(G, k): kept("gfs%d%d" % (G, k), [P, 512], U8) for G in range(2) for k in range(2)}
-        gt_codes = {(m, G): kept("gtc%d%d" % (m, G), [P, 256], U32) for m in range(4) for G in range(2)}
-        gt_scales = {(m, G): kept("gts%d%d" % (m, G), [P, 256], U8) for m in range(4) for G in range(2)}
-        h_codes, h_scales, w_codes, w_scales = {}, {}, {}, {}
-        xt_ps, h_t, h_grp, w_grp, gf_grp, gt_grp, dn, sums, coef, shift = {}, {}, {}, {}, {}, {}, {}, {}, {}, {}
-
-        tot_ps, dx_ps = {}, {}
+        gf_codes, gf_scales, gf_in = {}, {}, {}
+        gt_codes, gt_scales, gt_in = {}, {}, {}
+        w_codes, w_scales, w_in = {}, {}, {}
+        h_codes, h_scales, h_in = {}, {}, {}
+        ha_t, h_t, dn, sums, totals, coef, shift, dx_ps = {}, {}, {}, {}, {}, {}, {}, {}
 
         def quantize(codes, scales, values, fmt):
             nc.vector.quantize_mx(out=codes.bitcast(fmt), scales=scales, in_=values)
 
-        def transpose_x(b, tag, plain=False):
-            cols = slice((b % 2) * P, (b % 2 + 1) * P)
-            xt_ps[b] = bank(tag, [P, 2, 2, 2, P], BF16)
-            for G in range(2):
-                for u in range(2):
-                    for hf in range(2):
-                        nc.tensor.matmul(
-                            out=xt_ps[b][:, G, u, hf, :],
-                            lhsT=x_sb[b // 2, u][:, 2 * G + hf, cols],
-                            rhs=id_bf[:],
-                            start=True,
-                            stop=True,
-                            is_transpose=not plain,
-                        )
+        def copy_on_vector(out, in_):
+            nc.vector.tensor_copy(out=out, in_=in_)
 
-        def make_h(b, n_scalar):
-            h_t[b] = ring("h_t", [P, S], BF16, 4)
-            src = xt_ps[b][:].rearrange("p g u h q -> p (g u h q)")
-            if n_scalar:
-                nc.scalar.activation(
-                    out=h_t[b][:, 0:n_scalar],
-                    in_=src[:, 0:n_scalar],
-                    func=IDENT,
-                    scale=sc[:, b : b + 1],
-                    bias=sh[:, b : b + 1],
-                )
-            if n_scalar < S:
-                nc.vector.tensor_scalar(
-                    out=h_t[b][:, n_scalar:S],
-                    in0=src[:, n_scalar:S],
-                    scalar1=sc[:, b : b + 1],
-                    scalar2=sh[:, b : b + 1],
-                    op0=ALU.mult,
-                    op1=ALU.add,
-                )
-
-        def transpose_h(b, tag):
-            ps = bank(tag, [P, 2, 2, P], F32)
-            words = h_t[b][:].bitcast(F32)
-            for G in range(2):
-                for u in range(2):
-                    w0 = (2 * G + u) * P
-                    nc.tensor.transpose(ps[:, G, u, :], words[:, w0 : w0 + P], id_f[:])
-            h_grp[b] = ring("h_grp", [P, 2, 4 * P], BF16, 3)
-            nc.scalar.copy(
-                out=h_grp[b][:].bitcast(F32).rearrange("p g (c u) -> p g c u", u=2),
-                in_=ps[:].rearrange("p g u c -> p g c u"),
-            )
-
-        def quantize_h(b):
-            c, slot = divmod(b, 4)
-            cols = slice(slot * P, (slot + 1) * P)
-            for G in range(2):
-                if slot == 0:
-                    h_codes[c, G] = ring("h_codes%d" % G, [P, CH], U32, 3)
-                    h_scales[c, G] = ring("h_scales%d" % G, [P, CH], U8, 3)
-                quantize(h_codes[c, G][:, cols], h_scales[c, G][:, cols], h_grp[b][:, G, :], E4)
+        def copy_on_scalar(out, in_):
+            nc.scalar.copy(out=out, in_=in_)
 
         def transpose_g(G, k, tags):
-            gf_grp[G, k] = ring("gf_grp", [P, 2, 1024], BF16, 2)
+            gf_in[G, k] = ring("gf_in", [P, 2, 1024], BF16, 2)
             words = g_sb[G, k][:].bitcast(F32)
             for u in range(2):
                 ps = bank(tags[u], [P, 4, P], F32)
                 for e in range(2):
                     for w in range(2):
-                        nc.tensor.transpose(ps[:, 2 * e + w, :], words[:, 2 * e + u, w:256:2], id_f[:])
+                        nc.tensor.transpose(ps[:, 2 * e + w, :], words[:, 2 * e + u, w:256:2], ident[:])
                 nc.scalar.copy(
-                    out=gf_grp[G, k][:, u, :].bitcast(F32).rearrange("p (t m) -> p t m", m=4),
+                    out=gf_in[G, k][:, u, :].bitcast(F32).rearrange("p (t m) -> p t m", m=4),
                     in_=ps[:].rearrange("p m t -> p t m"),
                 )
 
         def quantize_gf(G, k):
-            quantize(gf_codes[G, k][:], gf_scales[G, k][:], gf_grp[G, k][:].rearrange("p u n -> p (u n)"), E5)
+            gf_codes[G, k] = kept("gf_codes%d_%d" % (G, k), [P, HALF], U32)
+            gf_scales[G, k] = kept("gf_scales%d_%d" % (G, k), [P, HALF], U8)
+            quantize(gf_codes[G, k][:], gf_scales[G, k][:], gf_in[G, k][:].rearrange("p u n -> p (u n)"), E5M2)
 
-        def move_on_gpsimd(out, in_):
-            nc.gpsimd.tensor_scalar(out=out, in0=in_, scalar1=1.0, scalar2=0.0, op0=ALU.mult, op1=ALU.add)
-
-        def move_on_vector(out, in_):
-            nc.vector.tensor_copy(out=out, in_=in_)
-
-        def move_on_scalar(out, in_):
-            nc.scalar.copy(out=out, in_=in_)
-
-        def interleave_g(m, G, move):
-            gt_grp[m, G] = ring("gt_grp", [P, 1024], BF16, 4)
+        def interleave_g(m, G, copy, shared=False):
+            gt_in[m, G] = ring("w_in", [P, 1024], BF16, 1) if shared else ring("gt_in", [P, 1024], BF16, 4)
             src = g_sb[G, m // 2][:, :, (m % 2) * 256 : (m % 2 + 1) * 256]
-            move(
-                gt_grp[m, G][:].rearrange("p (d i u e) -> p d u e i", i=4, u=2, e=2),
+            copy(
+                gt_in[m, G][:].rearrange("p (d i u e) -> p d u e i", i=4, u=2, e=2),
                 src.rearrange("p (e u) (d i) -> p d u e i", u=2, i=4),
             )
 
         def quantize_gt(m, G):
-            quantize(gt_codes[m, G][:], gt_scales[m, G][:], gt_grp[m, G][:], E5)
+            gt_codes[m, G] = kept("gt_codes%d_%d" % (m, G), [P, 256], U32)
+            gt_scales[m, G] = kept("gt_scales%d_%d" % (m, G), [P, 256], U8)
+            quantize(gt_codes[m, G][:], gt_scales[m, G][:], gt_in[m, G][:], E5M2)
 
-        def interleave_w(b, on_vector):
-            cols = slice((b % 2) * P, (b % 2 + 1) * P)
-            w_grp[b] = ring("w_grp", [P, 1024], BF16, 1)
-            src = w_sb[b // 2][:, :, :, cols]
-            if on_vector:
-                move_on_vector(
-                    w_grp[b][:].rearrange("p (k c i j) -> p k c j i", k=2, i=4, j=4),
-                    src.rearrange("p k j (c i) -> p k c j i", i=4),
-                )
-            else:
-                move_on_gpsimd(
-                    w_grp[b][:].rearrange("p (k c j) -> p k c j", k=2, j=4), src.rearrange("p k j c -> p k c j")
-                )
+        def w_columns(n, buffer):
+            w_in[n] = buffer
+            return w_sb[n // 2].rearrange("p k j (c e) -> p k j c e", e=2)[:, :, :, :, n % 2]
 
-        def quantize_w(b):
-            w_codes[b] = ring("w_codes", [P, 2 * P], U32, 3)
-            w_scales[b] = ring("w_scales", [P, 2 * P], U8, 3)
-            quantize(w_codes[b][:], w_scales[b][:], w_grp[b][:], E4)
+        def interleave_w_on_vector(n):
+            src = w_columns(n, ring("gt_in", [P, 1024], BF16, 4))
+            nc.vector.tensor_copy(
+                out=w_in[n][:].rearrange("p (k c i j) -> p k c j i", k=2, i=4, j=4),
+                in_=src.rearrange("p k j (c i) -> p k c j i", i=4),
+            )
 
-        def product_dh(b, G):
-            gam, e = b // 2, b % 2
-            if G == 0:
-                if e == 0:
-                    sums[gam] = ring("sums", [P, 8], F32, 2)
-                dn[b] = ring("dn", [P, S], F32, 6)
-            ps = bank("dh%d" % G, [P, 512], F32)
+        def interleave_w_on_gpsimd(n):
+            src = w_columns(n, ring("w_in", [P, 1024], BF16, 1))
+            nc.gpsimd.tensor_scalar(
+                out=w_in[n][:].rearrange("p (k c j) -> p k c j", k=2, j=4),
+                in0=src.rearrange("p k j c -> p k c j"),
+                scalar1=1.0,
+                scalar2=0.0,
+                op0=ALU.mult,
+                op1=ALU.add,
+            )
+
+        def quantize_w(n):
+            w_codes[n] = ring("w_codes", [P, 2 * P], U32, 4)
+            w_scales[n] = ring("w_scales", [P, 2 * P], U8, 4)
+            quantize(w_codes[n][:], w_scales[n][:], w_in[n][:], E4M3)
+
+        def transpose_ha(i, tag):
+            ps = bank(tag, [P, 2, 2, P], F32)
+            for u in range(2):
+                for f in range(2):
+                    words = ha_sb[i // 2, u][:, 2 * (i % 2) + f, :].bitcast(F32)
+                    nc.tensor.transpose(ps[:, u, f, :], words, ident[:])
+            pairs = ps[:].rearrange("p u f q -> p (u f q)").bitcast(BF16).rearrange("p (n e) -> p n e", e=2)
+            ha_t[i] = [pairs[:, :, e] for e in range(2)]
+
+        def make_h(i, parities_on_scalar):
+            h_t[i] = ring("h_t", [P, 2, HALF], BF16, 2)
+            for e in range(2):
+                mul, add = scale[:, i // 2, e : e + 1], offset[:, i // 2, e : e + 1]
+                if e < parities_on_scalar:
+                    nc.scalar.activation(out=h_t[i][:, e, :], in_=ha_t[i][e], func=IDENTITY, scale=mul, bias=add)
+                else:
+                    nc.vector.tensor_scalar(
+                        out=h_t[i][:, e, :], in0=ha_t[i][e], scalar1=mul, scalar2=add, op0=ALU.mult, op1=ALU.add
+                    )
+
+        def transpose_h(i):
+            ps = bank("hw", [P, 2, 2, P], F32)
+            for e in range(2):
+                words = h_t[i][:, e, :].bitcast(F32)
+                for u in range(2):
+                    nc.tensor.transpose(ps[:, e, u, :], words[:, u * P : (u + 1) * P], ident[:])
+            h_in[i] = ring("h_in", [P, 4 * DH], BF16, 2)
+            nc.scalar.copy(
+                out=h_in[i][:].bitcast(F32).rearrange("p (c m) -> p c m", m=4),
+                in_=ps[:].rearrange("p e u c -> p c (e u)"),
+            )
+
+        def quantize_h(i):
+            chunk, second, G = i // 4, (i // 2) % 2, i % 2
+            if not second:
+                h_codes[chunk, G] = ring("h_codes%d" % G, [P, CHUNK], U32, 2)
+                h_scales[chunk, G] = ring("h_scales%d" % G, [P, CHUNK], U8, 2)
+            cols = slice(second * DH, (second + 1) * DH)
+            quantize(h_codes[chunk, G][:, cols], h_scales[chunk, G][:, cols], h_in[i][:], E4M3)
+
+        def product_dh(i, e):
+            group, G = divmod(i, 2)
+            if e == 0:
+                if G == 0:
+                    sums[group] = ring("sums", [P, 8], F32, 2)
+                dn[i] = ring("dn", [P, 2, HALF], F32, 4)
+            n = 2 * group + e
+            ps = bank("dh%d" % e, [P, HALF], F32)
             for k in range(2):
                 nc.tensor.matmul_mx(
                     out=ps[:],
-                    lhsT=w_codes[b][:, k * P : (k + 1) * P].bitcast(E4),
-                    lhsT_scale=w_scales[b][:, k * P : (k + 1) * P],
-                    rhs=gf_codes[G, k][:].bitcast(E5),
+                    lhsT=w_codes[n][:, k * P : (k + 1) * P].bitcast(E4M3),
+                    lhsT_scale=w_scales[n][:, k * P : (k + 1) * P],
+                    rhs=gf_codes[G, k][:].bitcast(E5M2),
                     rhs_scale=gf_scales[G, k][:],
                     start=(k == 0),
                     stop=(k == 1),
                 )
             nc.scalar.activation(
-                out=dn[b][:, G * 512 : (G + 1) * 512],
+                out=dn[i][:, e, :],
                 in_=ps[:],
-                func=IDENT,
-                scale=sc[:, b : b + 1],
-                accum_out=sums[gam][:, 2 * e + G : 2 * e + G + 1],
+                func=IDENTITY,
+                scale=scale[:, group, e : e + 1],
+                accum_out=sums[group][:, 2 * G + e : 2 * G + e + 1],
             )
 
-        def product_dw(c, m, tags, moves, split=False):
-            stage = ring("dw_stage", [P, 2, CH], F32, 4)
-            rows = out_1[256 * m : 256 * (m + 1), c * CH : (c + 1) * CH].rearrange("(t p) c -> p t c", p=P)
+        def product_dw(chunk, m, tags, store_each=False, between=None):
+            stage = ring("dw_stage", [P, 2, CHUNK], F32, 5)
+            rows = out_1[256 * m : 256 * (m + 1), chunk * CHUNK : (chunk + 1) * CHUNK]
+            rows = rows.rearrange("(t p) c -> p t c", p=P)
+            tiles = [bank(tag, [P, CHUNK], F32) for tag in tags]
             for t in range(2):
-                ps = bank(tags[t], [P, CH], F32)
                 for G in range(2):
                     nc.tensor.matmul_mx(
-                        out=ps[:],
-                        lhsT=gt_codes[m, G][:, t * P : (t + 1) * P].bitcast(E5),
+                        out=tiles[t][:],
+                        lhsT=gt_codes[m, G][:, t * P : (t + 1) * P].bitcast(E5M2),
                         lhsT_scale=gt_scales[m, G][:, t * P : (t + 1) * P],
-                        rhs=h_codes[c, G][:].bitcast(E4),
-                        rhs_scale=h_scales[c, G][:],
+                        rhs=h_codes[chunk, G][:].bitcast(E4M3),
+                        rhs_scale=h_scales[chunk, G][:],
                         start=(G == 0),
                         stop=(G == 1),
                     )
-                moves[t](stage[:, t, :], ps[:])
-                if split:
+            for t in range(2):
+                nc.scalar.copy(out=stage[:, t, :], in_=tiles[t][:])
+                if store_each:
                     nc.sync.dma_start(out=rows[:, t, :], in_=stage[:, t, :])
-            if not split:
+                if between and t == 0:
+                    between()
+            if not store_each:
                 nc.sync.dma_start(out=rows, in_=stage[:])
 
-        def sum_dn_x(b, G):
-            gam, e = b // 2, b % 2
-            prod = ring("prod", [P, 512], F32, 2)
-            col = 4 + 2 * e + G
+        def sum_dn_ha(i, e):
+            group, G = divmod(i, 2)
+            products = ring("products", [P, HALF], F32, 2)
             nc.vector.scalar_tensor_tensor(
-                out=prod[:],
-                in0=xt_ps[b][:, G, :, :, :].rearrange("p u h q -> p (u h q)"),
-                scalar=mr[:, gam : gam + 1],
-                in1=dn[b][:, G * 512 : (G + 1) * 512],
+                out=products[:],
+                in0=ha_t[i][e],
+                scalar=mr[:, group : group + 1],
+                in1=dn[i][:, e, :],
                 op0=ALU.subtract,
                 op1=ALU.mult,
-                accum_out=sums[gam][:, col : col + 1],
+                accum_out=sums[group][:, 4 + 2 * G + e : 5 + 2 * G + e],
             )
 
-        def group_sums(gam, tag, n):
-            tot_ps[gam] = bank(tag, [P, n], F32)
-            nc.tensor.matmul(out=tot_ps[gam][:], lhsT=ones[:], rhs=sums[gam][:, 0:n], start=True, stop=True)
+        def group_totals(group, tag):
+            totals[group] = bank(tag, [P, 8], F32)
+            nc.tensor.matmul(out=totals[group][:], lhsT=ones[:], rhs=sums[group][:], start=True, stop=True)
 
-        def group_coefficients(gam, n):
-            coef[gam] = ring("coef", [P, 2], F32, 3)
-            terms = ring("terms", [P, 16], F32, 2)
+        def group_coefficients(group):
+            coef[group] = ring("coef", [P, 2], F32, 2)
+            terms = ring("terms", [P, 12], F32, 2)
             nc.vector.tensor_scalar(
-                out=terms[:, 0 : n - 4],
-                in0=tot_ps[gam][:, 4:n],
-                scalar1=ca[:, gam : gam + 1],
+                out=terms[:, 0:4],
+                in0=totals[group][:, 4:8],
+                scalar1=a_weight[:, group : group + 1],
                 scalar2=None,
                 op0=ALU.mult,
                 op1=ALU.add,
-                accum_out=coef[gam][:, 0:1],
+                accum_out=coef[group][:, 0:1],
             )
             nc.vector.scalar_tensor_tensor(
-                out=terms[:, 8 : 8 + n],
-                in0=tot_ps[gam][:],
+                out=terms[:, 4:12],
+                in0=totals[group][:],
                 scalar=1.0,
-                in1=cb[:, gam, 0:n],
+                in1=b_weights[:, group, :],
                 op0=ALU.mult,
                 op1=ALU.mult,
-                accum_out=coef[gam][:, 1:2],
+                accum_out=coef[group][:, 1:2],
             )
 
-        def make_shift(gam, G, u, on_scalar):
-            shift[gam, G, u] = ring("shift", [P, 2, DH], F32, 6)
-            src = x_sb[gam, u][:, 2 * G : 2 * G + 2, :]
+        def make_shift(i, u, on_scalar=False):
+            group, G = divmod(i, 2)
+            shift[i, u] = ring("shift", [P, 2, DH], F32, 6)
+            src, a, b = ha_sb[group, u][:, 2 * G : 2 * G + 2, :], coef[group][:, 0:1], coef[group][:, 1:2]
             if on_scalar:
-                nc.scalar.activation(
-                    out=shift[gam, G, u][:], in_=src, func=IDENT, scale=coef[gam][:, 0:1], bias=coef[gam][:, 1:2]
-                )
+                nc.scalar.activation(out=shift[i, u][:], in_=src, func=IDENTITY, scale=a, bias=b)
             else:
                 nc.gpsimd.tensor_scalar(
-                    out=shift[gam, G, u][:],
-                    in0=src,
-                    scalar1=coef[gam][:, 0:1],
-                    scalar2=coef[gam][:, 1:2],
-                    op0=ALU.mult,
-                    op1=ALU.add,
+                    out=shift[i, u][:], in0=src, scalar1=a, scalar2=b, op0=ALU.mult, op1=ALU.add
                 )
 
-        def transpose_dn(gam, G, u, tag):
-            dx_ps[gam, G, u] = bank(tag, [P, 2, DH], F32)
-            for hf in range(2):
-                t0 = G * 512 + u * 256 + hf * P
+        def transpose_dn(i, u, tag):
+            dx_ps[i, u] = bank(tag, [P, 2, 2, P], F32)
+            for f in range(2):
                 for e in range(2):
-                    nc.tensor.transpose(
-                        dx_ps[gam, G, u][:, hf, e * P : (e + 1) * P], dn[2 * gam + e][:, t0 : t0 + P], id_f[:]
-                    )
+                    t0 = u * 256 + f * P
+                    nc.tensor.transpose(dx_ps[i, u][:, f, e, :], dn[i][:, e, t0 : t0 + P], ident[:])
 
-        def finish_dx(gam, G, u):
-            stage = ring("dx_stage", [P, 2, DH], F32, 6)
-            nc.vector.tensor_tensor(out=stage[:], in0=dx_ps[gam, G, u][:], in1=shift[gam, G, u][:], op=ALU.add)
-            nc.sync.dma_start(out=oa[:, u, 2 * G : 2 * G + 2, gam * DH : (gam + 1) * DH], in_=stage[:])
+        def finish_dx(i, u):
+            group, G = divmod(i, 2)
+            stage = ring("dx_stage", [P, 2, DH], F32, 8)
+            nc.vector.tensor_tensor(
+                out=stage[:].rearrange("p f (c e) -> p f c e", e=2),
+                in0=dx_ps[i, u][:].rearrange("p f e c -> p f c e"),
+                in1=shift[i, u][:].rearrange("p f (c e) -> p f c e", e=2),
+                op=ALU.add,
+            )
+            nc.sync.dma_start(out=dx_hbm[:, u, 2 * G : 2 * G + 2, group * DH : (group + 1) * DH], in_=stage[:])
 
-        interleave_g(0, 0, move_on_scalar)
-        interleave_g(1, 0, move_on_vector)
-        transpose_g(0, 0, ("o0", "o1"))
-        interleave_g(2, 0, move_on_scalar)
+        interleave_g(0, 0, copy_on_scalar)
+        interleave_g(1, 0, copy_on_vector)
+        transpose_g(0, 0, ("dx0", "dx1"))
+        interleave_g(2, 0, copy_on_scalar)
         quantize_gt(1, 0)
-        interleave_g(3, 0, move_on_vector)
+        interleave_g(3, 0, copy_on_vector)
         quantize_gt(0, 0)
-        constants_0()
+        constants_spread()
         quantize_gt(3, 0)
-        constants_1()
+        constants_scale()
         transpose_g(0, 1, ("dw0", "dw1"))
         quantize_gf(0, 0)
-        constants_2()
-        interleave_g(0, 1, move_on_vector)
-        constants_3()
+        constants_mu()
+        interleave_g(0, 1, copy_on_vector)
+        constants_offset()
         quantize_gt(2, 0)
-        interleave_g(1, 1, move_on_vector)
+        interleave_g(1, 1, copy_on_vector)
         quantize_gt(0, 1)
         quantize_gf(0, 1)
-        transpose_g(1, 0, ("o0", "o1"))
-        interleave_w(0, True)
         quantize_gt(1, 1)
+        transpose_g(1, 0, ("dx0", "dx1"))
+        interleave_w_on_vector(0)
+        interleave_w_on_vector(1)
         quantize_w(0)
-        transpose_g(1, 1, ("xt", "hw"))
+        quantize_w(1)
+        transpose_g(1, 1, ("ha", "hw"))
+        transpose_ha(0, "dw0")
         quantize_gf(1, 0)
-        interleave_w(1, True)
-        product_dh(0, 0)
-        transpose_x(0, "dw0")
+        interleave_g(2, 1, copy_on_vector)
         quantize_gf(1, 1)
 
-        DW0 = 4
-        late_loads = {1: (load_w, 4, 2), 2: (load_x, 4, 2), 3: (load_w, 6, 2), 4: (load_x, 6, 2)}
-        LAST = NB - 1
-        on_scalar = (move_on_scalar, move_on_scalar)
+        late_loads = {3: load_w, 4: load_ha}
+        last = STEPS - 1
 
-        for i in range(NB):
+        for i in range(STEPS):
+            early = i < DW_LAG
             stats = i >= 2 and i % 2 == 0
-            early = i < DW0
             if i in late_loads:
-                late_loads[i][0](*late_loads[i][1:])
-            if i >= 1:
+                late_loads[i](6, 2)
+            if i == 0:
+                interleave_g(3, 1, copy_on_vector, True)
+                quantize_gt(2, 1)
+                interleave_w_on_vector(3)
+                quantize_gt(3, 1)
+                interleave_w_on_gpsimd(2)
+            if i == 1:
+                quantize_h(0)
+                quantize_w(3)
+                quantize_w(2)
+            if 2 <= i < STEPS - 3:
                 quantize_h(i - 1)
-            if i < 2:
-                interleave_g(i + 2, 1, move_on_vector)
-            if i + 1 < NB:
-                quantize_w(i + 1)
-            if i < 2:
-                quantize_gt(i + 2, 1)
-            if i + 2 < NB:
-                interleave_w(i + 2, False)
+                quantize_w(i + 2)
+            if 1 <= i < STEPS - 3:
+                interleave_w_on_gpsimd(i + 3)
             if i >= 3:
-                finish_dx((i - 3) // 2, (i - 3) % 2, 1)
-            make_h(i, S if early else H_ON_SCALAR)
-            if i > 0:
-                product_dh(i, 0)
+                finish_dx(i - 3, 1)
+            make_h(i, 2 if early else 1)
+            if i >= STEPS - 3:
+                quantize_h(i - 1)
+                if i + 2 < STEPS:
+                    quantize_w(i + 2)
+            product_dh(i, 0)
             product_dh(i, 1)
             if stats:
-                group_sums(i // 2 - 1, "hw", 8)
-            if i == LAST:
-                transpose_h(i, "hw")
+                group_totals(i // 2 - 1, "hw")
             if not early:
-                product_dw((i - DW0) // 4, (i - DW0) % 4, ("dw0", "dw1"), on_scalar)
+                between = (lambda: transpose_h(last)) if i == last else None
+                product_dw((i - DW_LAG) // 4, (i - DW_LAG) % 4, ("dw0", "dw1"), i == last, between)
             if stats:
-                group_coefficients(i // 2 - 1, 8)
-            sum_dn_x(i, 0)
+                group_coefficients(i // 2 - 1)
+            sum_dn_ha(i, 0)
             if i >= 2:
                 for u in range(2):
-                    make_shift((i - 2) // 2, i % 2, u, False)
-            sum_dn_x(i, 1)
+                    make_shift(i - 2, u, early and u == 0)
+            sum_dn_ha(i, 1)
             if early:
-                transpose_x(i + 1, "dw%d" % ((i + 1) % 2) if i + 1 < DW0 else "xt")
-            if i < LAST:
-                transpose_h(i, "hw")
-            else:
-                quantize_h(LAST)
+                transpose_ha(i + 1, "dw%d" % ((i + 1) % 2) if i + 1 < DW_LAG else "ha")
+            if i < last:
+                transpose_h(i)
             if i >= 2:
                 for u in range(2):
-                    transpose_dn((i - 2) // 2, i % 2, u, "o%d" % u)
-                finish_dx((i - 2) // 2, i % 2, 0)
-            if not early and i < LAST:
-                transpose_x(i + 1, "xt")
+                    transpose_dn(i - 2, u, "dx%d" % u)
+                finish_dx(i - 2, 0)
+            if not early and i < last:
+                transpose_ha(i + 1, "ha")
 
-        gam = H - 1
-        group_sums(gam, "xt", 8)
-        group_coefficients(gam, 8)
-        finish_dx(gam - 1, 1, 1)
-        order = [(0, 0), (1, 0), (0, 1), (1, 1)]
-        for G, u in order:
-            make_shift(gam, G, u, False)
-        product_dw(3, 0, ("dh0", "dh1"), on_scalar)
-        product_dw(3, 1, ("dw0", "dw1"), on_scalar)
-        for n, (G, u) in enumerate(order):
-            transpose_dn(gam, G, u, ("hw", "o0", "xt", "o1")[n])
-            finish_dx(gam, G, u)
-        product_dw(3, 2, ("dh0", "dh1"), on_scalar)
-        product_dw(3, 3, ("dw0", "dw1"), on_scalar, split=True)
+        quantize_h(last)
+        for u in range(2):
+            transpose_dn(last - 1, u, "dh%d" % u)
+        group_totals(H - 1, "ha")
+        group_coefficients(H - 1)
+        finish_dx(last - 2, 1)
+        for i in (last - 1, last):
+            for u in range(2):
+                make_shift(i, u)
+        product_dw(3, 0, ("dw0", "dw1"), True)
+        for u in range(2):
+            finish_dx(last - 1, u)
+        product_dw(3, 1, ("ha", "dx1"))
+        for u in range(2):
+            transpose_dn(last, u, ("hw", "dx0")[u])
+            finish_dx(last, u)
+        product_dw(3, 2, ("dw0", "dw1"))
+        product_dw(3, 3, ("dh0", "dh1"), store_each=True)

@@ -49,12 +49,14 @@ def tile_mlstmblock_pb_v_kernel(
         def bank(tag, shape, dtype):
             return psum.tile(shape, dtype, name=tag, tag=tag)
 
-        wb_rows = kept("wb_rows", [P, DH], BF16)
+        wb_rows = kept("wb_rows", [P, P], BF16)
         mr_col = kept("mr_col", [P, 8], F32)
         nc.vector.memset(wb_rows[:], 0.0)
         nc.vector.memset(mr_col[:, 0:1], 0.0)
         ident = kept("ident", [P, P], F32)
         make_identity(nc, ident[:])
+        ident_bf = kept("ident_bf", [P, P], BF16)
+        make_identity(nc, ident_bf[:])
         ones = kept("ones", [P, P], F32)
         nc.scalar.activation(out=ones[:], in_=ident[:], func=IDENTITY, scale=0.0, bias=1.0)
 
@@ -80,8 +82,8 @@ def tile_mlstmblock_pb_v_kernel(
                 nc.sync.dma_start(out=g_sb[G, k][:], in_=g_hbm[:, G, :, k * HALF : (k + 1) * HALF])
 
         load_g(0)
-        nc.sync.dma_start(out=wb_rows[0:H, :], in_=gn_w.rearrange("(h c) -> h c", c=DH))
-        nc.sync.dma_start(out=wb_rows[H : 2 * H, :], in_=gn_b.rearrange("(h c) -> h c", c=DH))
+        nc.sync.dma_start(out=wb_rows[0 : 2 * H, :], in_=gn_w.rearrange("(n c) -> n c", c=P))
+        nc.sync.dma_start(out=wb_rows[2 * H : 4 * H, :], in_=gn_b.rearrange("(n c) -> n c", c=P))
         with nc.allow_non_contiguous_dma(reason="one float32 value to a partition"):
             nc.sync.dma_start(out=mr_col[0:H, 0:1], in_=mu.rearrange("b h -> h b"))
             nc.sync.dma_start(out=mr_col[H : 2 * H, 0:1], in_=rstd.rearrange("b h -> h b"))
@@ -108,9 +110,9 @@ def tile_mlstmblock_pb_v_kernel(
             return cols.unsqueeze(2).to_broadcast([P, H, n])
 
         def constants_spread():
-            ps = bank("ha", [P, P], F32)
-            nc.tensor.transpose(ps[:], wb_rows[:].bitcast(F32), ident[:])
-            pairs = ps[:].bitcast(BF16).rearrange("p (r e) -> p r e", e=2)
+            ps = bank("ha", [P, P], BF16)
+            nc.tensor.transpose(ps[:], wb_rows[:], ident_bf[:])
+            pairs = ps[:].rearrange("p (r e) -> p r e", e=2)
             wb_t["w"], wb_t["b"] = pairs[:, 0:H, :], pairs[:, H : 2 * H, :]
             mr_ps = bank("hw", [P, P], F32)
             nc.tensor.transpose(mr_ps[:], mr_col[:, 0:1].to_broadcast([P, P]), ident[:])
@@ -138,7 +140,7 @@ def tile_mlstmblock_pb_v_kernel(
         gf_codes, gf_scales, gf_in = {}, {}, {}
         gt_codes, gt_scales, gt_in = {}, {}, {}
         w_codes, w_scales, w_in = {}, {}, {}
-        h_codes, h_scales, h_in = {}, {}, {}
+        h_codes, h_scales, pair_in, pair_codes, pair_scales = {}, {}, {}, {}, {}
         ha_t, h_t, dn, sums, totals, coef, shift, dx_ps = {}, {}, {}, {}, {}, {}, {}, {}
 
         def quantize(codes, scales, values, fmt):
@@ -169,7 +171,7 @@ def tile_mlstmblock_pb_v_kernel(
             quantize(gf_codes[G, k][:], gf_scales[G, k][:], gf_in[G, k][:].rearrange("p u n -> p (u n)"), E5M2)
 
         def interleave_g(m, G, copy, shared=False):
-            gt_in[m, G] = ring("w_in", [P, 1024], BF16, 1) if shared else ring("gt_in", [P, 1024], BF16, 4)
+            gt_in[m, G] = ring("pair_in", [P, 1024], BF16, 1) if shared else ring("gt_in", [P, 1024], BF16, 4)
             src = g_sb[G, m // 2][:, :, (m % 2) * 256 : (m % 2 + 1) * 256]
             copy(
                 gt_in[m, G][:].rearrange("p (d i u e) -> p d u e i", i=4, u=2, e=2),
@@ -181,41 +183,46 @@ def tile_mlstmblock_pb_v_kernel(
             gt_scales[m, G] = kept("gt_scales%d_%d" % (m, G), [P, 256], U8)
             quantize(gt_codes[m, G][:], gt_scales[m, G][:], gt_in[m, G][:], E5M2)
 
-        def w_columns(n, buffer):
-            w_in[n] = buffer
-            return w_sb[n // 2].rearrange("p k j (c e) -> p k j c e", e=2)[:, :, :, :, n % 2]
+        def w_columns(n):
+            return w_sb[n // 2][:, :, :, (n % 2) * P : (n % 2 + 1) * P]
 
         def interleave_w_on_vector(n):
-            src = w_columns(n, ring("gt_in", [P, 1024], BF16, 4))
+            w_in[n] = ring("gt_in", [P, 1024], BF16, 4)
             nc.vector.tensor_copy(
                 out=w_in[n][:].rearrange("p (k c i j) -> p k c j i", k=2, i=4, j=4),
-                in_=src.rearrange("p k j (c i) -> p k c j i", i=4),
+                in_=w_columns(n).rearrange("p k j (c i) -> p k c j i", i=4),
             )
 
-        def interleave_w_on_gpsimd(n):
-            src = w_columns(n, ring("w_in", [P, 1024], BF16, 1))
+        def quantize_w(n):
+            w_codes[n] = kept("w_codes%d" % n, [P, 2 * P], U32)[:]
+            w_scales[n] = kept("w_scales%d" % n, [P, 2 * P], U8)[:]
+            quantize(w_codes[n], w_scales[n], w_in[n][:], E4M3)
+
+        def open_pair(i):
+            pair_in[i] = ring("pair_in", [P, 2, 1024], BF16, 1)
+
+        def h_first(i):
+            return (i // 2) % 2
+
+        def interleave_w_on_gpsimd(n, i):
+            open_pair(i)
             nc.gpsimd.tensor_scalar(
-                out=w_in[n][:].rearrange("p (k c j) -> p k c j", k=2, j=4),
-                in0=src.rearrange("p k j c -> p k c j"),
+                out=pair_in[i][:, h_first(i), :].rearrange("p (k c j) -> p k c j", k=2, j=4),
+                in0=w_columns(n).rearrange("p k j c -> p k c j"),
                 scalar1=1.0,
                 scalar2=0.0,
                 op0=ALU.mult,
                 op1=ALU.add,
             )
 
-        def quantize_w(n):
-            w_codes[n] = ring("w_codes", [P, 2 * P], U32, 4)
-            w_scales[n] = ring("w_scales", [P, 2 * P], U8, 4)
-            quantize(w_codes[n][:], w_scales[n][:], w_in[n][:], E4M3)
-
         def transpose_ha(i, tag):
-            ps = bank(tag, [P, 2, 2, P], F32)
-            for u in range(2):
-                for f in range(2):
-                    words = ha_sb[i // 2, u][:, 2 * (i % 2) + f, :].bitcast(F32)
-                    nc.tensor.transpose(ps[:, u, f, :], words, ident[:])
-            pairs = ps[:].rearrange("p u f q -> p (u f q)").bitcast(BF16).rearrange("p (n e) -> p n e", e=2)
-            ha_t[i] = [pairs[:, :, e] for e in range(2)]
+            ps = bank(tag, [P, 2, 2, 2, P], BF16)
+            for e in range(2):
+                for u in range(2):
+                    for f in range(2):
+                        block = ha_sb[i // 2, u][:, 2 * (i % 2) + f, e * P : (e + 1) * P]
+                        nc.tensor.transpose(ps[:, e, u, f, :], block, ident_bf[:])
+            ha_t[i] = [ps[:, e, :, :, :].rearrange("p u f q -> p (u f q)") for e in range(2)]
 
         def make_h(i, parities_on_scalar):
             h_t[i] = ring("h_t", [P, 2, HALF], BF16, 2)
@@ -234,19 +241,32 @@ def tile_mlstmblock_pb_v_kernel(
                 words = h_t[i][:, e, :].bitcast(F32)
                 for u in range(2):
                     nc.tensor.transpose(ps[:, e, u, :], words[:, u * P : (u + 1) * P], ident[:])
-            h_in[i] = ring("h_in", [P, 4 * DH], BF16, 2)
+            if i not in pair_in:
+                open_pair(i)
             nc.scalar.copy(
-                out=h_in[i][:].bitcast(F32).rearrange("p (c m) -> p c m", m=4),
-                in_=ps[:].rearrange("p e u c -> p c (e u)"),
+                out=pair_in[i][:, 1 - h_first(i), :].bitcast(F32).rearrange("p (e c u) -> p e c u", e=2, u=2),
+                in_=ps[:].rearrange("p e u c -> p e c u"),
             )
 
-        def quantize_h(i):
-            chunk, second, G = i // 4, (i // 2) % 2, i % 2
+        def quantize_pair(i, n=None):
+            chunk, second, G = i // 4, h_first(i), i % 2
             if not second:
-                h_codes[chunk, G] = ring("h_codes%d" % G, [P, CHUNK], U32, 2)
-                h_scales[chunk, G] = ring("h_scales%d" % G, [P, CHUNK], U8, 2)
-            cols = slice(second * DH, (second + 1) * DH)
-            quantize(h_codes[chunk, G][:, cols], h_scales[chunk, G][:, cols], h_in[i][:], E4M3)
+                pair_codes[chunk, G] = ring("pair_codes%d" % G, [P, 4, DH], U32, 2)
+                pair_scales[chunk, G] = ring("pair_scales%d" % G, [P, 4, DH], U8, 2)
+                h_codes[chunk, G] = pair_codes[chunk, G][:, 1:3, :].rearrange("p a c -> p (a c)")
+                h_scales[chunk, G] = pair_scales[chunk, G][:, 1:3, :].rearrange("p a c -> p (a c)")
+            codes, scales = pair_codes[chunk, G], pair_scales[chunk, G]
+            if n is None:
+                quantize(codes[:, 1 + second, :], scales[:, 1 + second, :], pair_in[i][:, 1 - second, :], E4M3)
+            else:
+                w_codes[n], w_scales[n] = codes[:, 3 * second, :], scales[:, 3 * second, :]
+                both = slice(2 * second, 2 * second + 2)
+                quantize(
+                    codes[:, both, :].rearrange("p a c -> p (a c)"),
+                    scales[:, both, :].rearrange("p a c -> p (a c)"),
+                    pair_in[i][:].rearrange("p a c -> p (a c)"),
+                    E4M3,
+                )
 
         def product_dh(i, e):
             group, G = divmod(i, 2)
@@ -285,8 +305,8 @@ def tile_mlstmblock_pb_v_kernel(
                         out=tiles[t][:],
                         lhsT=gt_codes[m, G][:, t * P : (t + 1) * P].bitcast(E5M2),
                         lhsT_scale=gt_scales[m, G][:, t * P : (t + 1) * P],
-                        rhs=h_codes[chunk, G][:].bitcast(E4M3),
-                        rhs_scale=h_scales[chunk, G][:],
+                        rhs=h_codes[chunk, G].bitcast(E4M3),
+                        rhs_scale=h_scales[chunk, G],
                         start=(G == 0),
                         stop=(G == 1),
                     )
@@ -360,10 +380,7 @@ def tile_mlstmblock_pb_v_kernel(
             group, G = divmod(i, 2)
             stage = ring("dx_stage", [P, 2, DH], F32, 8)
             nc.vector.tensor_tensor(
-                out=stage[:].rearrange("p f (c e) -> p f c e", e=2),
-                in0=dx_ps[i, u][:].rearrange("p f e c -> p f c e"),
-                in1=shift[i, u][:].rearrange("p f (c e) -> p f c e", e=2),
-                op=ALU.add,
+                out=stage[:], in0=dx_ps[i, u][:].rearrange("p f e c -> p f (e c)"), in1=shift[i, u][:], op=ALU.add
             )
             nc.sync.dma_start(out=dx_hbm[:, u, 2 * G : 2 * G + 2, group * DH : (group + 1) * DH], in_=stage[:])
 
@@ -411,23 +428,19 @@ def tile_mlstmblock_pb_v_kernel(
                 quantize_gt(2, 1)
                 interleave_w_on_vector(3)
                 quantize_gt(3, 1)
-                interleave_w_on_gpsimd(2)
+                interleave_w_on_gpsimd(2, 0)
             if i == 1:
-                quantize_h(0)
                 quantize_w(3)
-                quantize_w(2)
+                quantize_pair(0, 2)
             if 2 <= i < STEPS - 3:
-                quantize_h(i - 1)
-                quantize_w(i + 2)
+                quantize_pair(i - 1, i + 2)
             if 1 <= i < STEPS - 3:
-                interleave_w_on_gpsimd(i + 3)
+                interleave_w_on_gpsimd(i + 3, i)
             if i >= 3:
                 finish_dx(i - 3, 1)
             make_h(i, 2 if early else 1)
             if i >= STEPS - 3:
-                quantize_h(i - 1)
-                if i + 2 < STEPS:
-                    quantize_w(i + 2)
+                quantize_pair(i - 1, i + 2 if i + 2 < STEPS else None)
             product_dh(i, 0)
             product_dh(i, 1)
             if stats:
@@ -453,7 +466,7 @@ def tile_mlstmblock_pb_v_kernel(
             if not early and i < last:
                 transpose_ha(i + 1, "ha")
 
-        quantize_h(last)
+        quantize_pair(last)
         for u in range(2):
             transpose_dn(last - 1, u, "dh%d" % u)
         group_totals(H - 1, "ha")

@@ -49,14 +49,12 @@ def tile_mlstmblock_pb_v_kernel(
         def bank(tag, shape, dtype):
             return psum.tile(shape, dtype, name=tag, tag=tag)
 
-        wb_rows = kept("wb_rows", [P, P], BF16)
+        wb_rows = kept("wb_rows", [P, DH], BF16)
         mr_col = kept("mr_col", [P, 8], F32)
         nc.vector.memset(wb_rows[:], 0.0)
         nc.vector.memset(mr_col[:, 0:1], 0.0)
         ident = kept("ident", [P, P], F32)
         make_identity(nc, ident[:])
-        ident_bf = kept("ident_bf", [P, P], BF16)
-        make_identity(nc, ident_bf[:])
         ones = kept("ones", [P, P], F32)
         nc.scalar.activation(out=ones[:], in_=ident[:], func=IDENTITY, scale=0.0, bias=1.0)
 
@@ -82,8 +80,8 @@ def tile_mlstmblock_pb_v_kernel(
                 nc.sync.dma_start(out=g_sb[G, k][:], in_=g_hbm[:, G, :, k * HALF : (k + 1) * HALF])
 
         load_g(0)
-        nc.sync.dma_start(out=wb_rows[0 : 2 * H, :], in_=gn_w.rearrange("(n c) -> n c", c=P))
-        nc.sync.dma_start(out=wb_rows[2 * H : 4 * H, :], in_=gn_b.rearrange("(n c) -> n c", c=P))
+        nc.sync.dma_start(out=wb_rows[0:H, :], in_=gn_w.rearrange("(h c) -> h c", c=DH))
+        nc.sync.dma_start(out=wb_rows[H : 2 * H, :], in_=gn_b.rearrange("(h c) -> h c", c=DH))
         with nc.allow_non_contiguous_dma(reason="one float32 value to a partition"):
             nc.sync.dma_start(out=mr_col[0:H, 0:1], in_=mu.rearrange("b h -> h b"))
             nc.sync.dma_start(out=mr_col[H : 2 * H, 0:1], in_=rstd.rearrange("b h -> h b"))
@@ -110,9 +108,9 @@ def tile_mlstmblock_pb_v_kernel(
             return cols.unsqueeze(2).to_broadcast([P, H, n])
 
         def constants_spread():
-            ps = bank("ha", [P, P], BF16)
-            nc.tensor.transpose(ps[:], wb_rows[:], ident_bf[:])
-            pairs = ps[:].rearrange("p (r e) -> p r e", e=2)
+            ps = bank("ha", [P, P], F32)
+            nc.tensor.transpose(ps[:], wb_rows[:].bitcast(F32), ident[:])
+            pairs = ps[:].bitcast(BF16).rearrange("p (r e) -> p r e", e=2)
             wb_t["w"], wb_t["b"] = pairs[:, 0:H, :], pairs[:, H : 2 * H, :]
             mr_ps = bank("hw", [P, P], F32)
             nc.tensor.transpose(mr_ps[:], mr_col[:, 0:1].to_broadcast([P, P]), ident[:])
@@ -184,13 +182,13 @@ def tile_mlstmblock_pb_v_kernel(
             quantize(gt_codes[m, G][:], gt_scales[m, G][:], gt_in[m, G][:], E5M2)
 
         def w_columns(n):
-            return w_sb[n // 2][:, :, :, (n % 2) * P : (n % 2 + 1) * P]
+            return w_sb[n // 2][:, n % 2, :, :]
 
         def interleave_w_on_vector(n):
             w_in[n] = ring("gt_in", [P, 1024], BF16, 4)
             nc.vector.tensor_copy(
-                out=w_in[n][:].rearrange("p (k c i j) -> p k c j i", k=2, i=4, j=4),
-                in_=w_columns(n).rearrange("p k j (c i) -> p k c j i", i=4),
+                out=w_in[n][:].rearrange("p (e c i j) -> p c e i j", e=2, i=2, j=4),
+                in_=w_columns(n).rearrange("p j (c i e) -> p c e i j", i=2, e=2),
             )
 
         def quantize_w(n):
@@ -207,8 +205,8 @@ def tile_mlstmblock_pb_v_kernel(
         def interleave_w_on_gpsimd(n, i):
             open_pair(i)
             nc.gpsimd.tensor_scalar(
-                out=pair_in[i][:, h_first(i), :].rearrange("p (k c j) -> p k c j", k=2, j=4),
-                in0=w_columns(n).rearrange("p k j c -> p k c j"),
+                out=pair_in[i][:, h_first(i), :].rearrange("p (e c j) -> p c e j", e=2, j=4),
+                in0=w_columns(n).rearrange("p j (c e) -> p c e j", e=2),
                 scalar1=1.0,
                 scalar2=0.0,
                 op0=ALU.mult,
@@ -216,13 +214,13 @@ def tile_mlstmblock_pb_v_kernel(
             )
 
         def transpose_ha(i, tag):
-            ps = bank(tag, [P, 2, 2, 2, P], BF16)
-            for e in range(2):
-                for u in range(2):
-                    for f in range(2):
-                        block = ha_sb[i // 2, u][:, 2 * (i % 2) + f, e * P : (e + 1) * P]
-                        nc.tensor.transpose(ps[:, e, u, f, :], block, ident_bf[:])
-            ha_t[i] = [ps[:, e, :, :, :].rearrange("p u f q -> p (u f q)") for e in range(2)]
+            ps = bank(tag, [P, 2, 2, P], F32)
+            for u in range(2):
+                for f in range(2):
+                    words = ha_sb[i // 2, u][:, 2 * (i % 2) + f, :].bitcast(F32)
+                    nc.tensor.transpose(ps[:, u, f, :], words, ident[:])
+            pairs = ps[:].rearrange("p u f q -> p (u f q)").bitcast(BF16).rearrange("p (n e) -> p n e", e=2)
+            ha_t[i] = [pairs[:, :, e] for e in range(2)]
 
         def make_h(i, parities_on_scalar):
             h_t[i] = ring("h_t", [P, 2, HALF], BF16, 2)
@@ -274,13 +272,13 @@ def tile_mlstmblock_pb_v_kernel(
                 if G == 0:
                     sums[group] = ring("sums", [P, 8], F32, 2)
                 dn[i] = ring("dn", [P, 2, HALF], F32, 4)
-            n = 2 * group + e
             ps = bank("dh%d" % e, [P, HALF], F32)
             for k in range(2):
+                n = 2 * group + k
                 nc.tensor.matmul_mx(
                     out=ps[:],
-                    lhsT=w_codes[n][:, k * P : (k + 1) * P].bitcast(E4M3),
-                    lhsT_scale=w_scales[n][:, k * P : (k + 1) * P],
+                    lhsT=w_codes[n][:, e * P : (e + 1) * P].bitcast(E4M3),
+                    lhsT_scale=w_scales[n][:, e * P : (e + 1) * P],
                     rhs=gf_codes[G, k][:].bitcast(E5M2),
                     rhs_scale=gf_scales[G, k][:],
                     start=(k == 0),
@@ -311,7 +309,10 @@ def tile_mlstmblock_pb_v_kernel(
                         stop=(G == 1),
                     )
             for t in range(2):
-                nc.scalar.copy(out=stage[:, t, :], in_=tiles[t][:])
+                nc.scalar.copy(
+                    out=stage[:, t, :].rearrange("p (g c e) -> p g c e", g=2, e=2),
+                    in_=tiles[t][:].rearrange("p (g e c) -> p g c e", g=2, e=2),
+                )
                 if store_each:
                     nc.sync.dma_start(out=rows[:, t, :], in_=stage[:, t, :])
                 if between and t == 0:
@@ -380,7 +381,10 @@ def tile_mlstmblock_pb_v_kernel(
             group, G = divmod(i, 2)
             stage = ring("dx_stage", [P, 2, DH], F32, 8)
             nc.vector.tensor_tensor(
-                out=stage[:], in0=dx_ps[i, u][:].rearrange("p f e c -> p f (e c)"), in1=shift[i, u][:], op=ALU.add
+                out=stage[:].rearrange("p f (c e) -> p f c e", e=2),
+                in0=dx_ps[i, u][:].rearrange("p f e c -> p f c e"),
+                in1=shift[i, u][:].rearrange("p f (c e) -> p f c e", e=2),
+                op=ALU.add,
             )
             nc.sync.dma_start(out=dx_hbm[:, u, 2 * G : 2 * G + 2, group * DH : (group + 1) * DH], in_=stage[:])
 

from contextlib import ExitStack

import concourse.mybir as mybir
from concourse.masks import make_identity

S, DM, H, DH = 1024, 1024, 8, 256
DI = H * DH
FLOPS = 2 * 2 * S * DM * DI
BYTES = 2 * (S * DI + DM * DI + S * DM + 2 * DI) + 4 * 2 * H + 4 * (S * DI + DM * DI)

F32 = mybir.dt.float32
BF16 = mybir.dt.bfloat16
U32 = mybir.dt.uint32
U8 = mybir.dt.uint8
E4M3 = mybir.dt.float8_e4m3fn_x4
E5M2 = mybir.dt.float8_e5m2_x4
ALU = mybir.AluOpType
IDENTITY = mybir.ActivationFunctionType.Identity

P = 128
HALF = 512
CHUNK = 512
STEPS = 2 * H
DW_LAG = 4
INV_N = 1.0 / (S * DH)


def tile_mlstmblock_pb_v_kernel(
    tc, h_attn, gn_w, gn_b, W_out, x, skip_scale, mu, rstd, grad_out, out_0, out_1
):
    nc = tc.nc
    ha_hbm = h_attn.rearrange("b (s q u) c -> q u (b s) c", q=P, u=2)
    dx_hbm = out_0.rearrange("b (s q u) c -> q u (b s) c", q=P, u=2)
    g_hbm = grad_out.rearrange("b (g p j) d -> p (b g) j d", p=P, j=4)
    w_hbm = W_out.rearrange("(k p j) c -> p k j c", p=P, j=4)

    with ExitStack() as ctx:
        keep = ctx.enter_context(tc.tile_pool(name="keep", bufs=1))
        work = ctx.enter_context(tc.tile_pool(name="work", bufs=2))
        psum = ctx.enter_context(tc.psum_pool(name="psum", bufs=1))
        ctx.enter_context(tc.manual_schedule())

        def kept(name, shape, dtype):
            return keep.tile(shape, dtype, name=name, tag=name, align_bytes=64)

        def ring(name, shape, dtype, bufs):
            return work.tile(shape, dtype, name=name, tag=name, bufs=bufs, align_bytes=64)

        def bank(tag, shape, dtype):
            return psum.tile(shape, dtype, name=tag, tag=tag)

        wb_rows = kept("wb_rows", [P, DH], BF16)
        mr_col = kept("mr_col", [P, 8], F32)
        nc.vector.memset(wb_rows[:], 0.0)
        nc.vector.memset(mr_col[:, 0:1], 0.0)
        ident = kept("ident", [P, P], F32)
        make_identity(nc, ident[:])
        ones = kept("ones", [P, P], F32)
        nc.scalar.activation(out=ones[:], in_=ident[:], func=IDENTITY, scale=0.0, bias=1.0)

        ha_sb, w_sb, g_sb = {}, {}, {}

        def load_ha(first, n):
            for u in range(2):
                t = kept("ha%d_%d" % (first, u), [P, 4, n * DH], BF16)
                nc.sync.dma_start(out=t[:], in_=ha_hbm[:, u, :, first * DH : (first + n) * DH])
                for j in range(n):
                    ha_sb[first + j, u] = t[:, :, j * DH : (j + 1) * DH]

        def load_w(first, n):
            t = kept("w%d" % first, [P, 2, 4, n * DH], BF16)
            for k in range(2):
                nc.sync.dma_start(out=t[:, k, :, :], in_=w_hbm[:, k, :, first * DH : (first + n) * DH])
            for j in range(n):
                w_sb[first + j] = t[:, :, :, j * DH : (j + 1) * DH]

        def load_g(G):
            for k in range(2):
                g_sb[G, k] = kept("g%d_%d" % (G, k), [P, 4, HALF], BF16)
                nc.sync.dma_start(out=g_sb[G, k][:], in_=g_hbm[:, G, :, k * HALF : (k + 1) * HALF])

        load_g(0)
        nc.sync.dma_start(out=wb_rows[0:H, :], in_=gn_w.rearrange("(h c) -> h c", c=DH))
        nc.sync.dma_start(out=wb_rows[H : 2 * H, :], in_=gn_b.rearrange("(h c) -> h c", c=DH))
        with nc.allow_non_contiguous_dma(reason="one float32 value to a partition"):
            nc.sync.dma_start(out=mr_col[0:H, 0:1], in_=mu.rearrange("b h -> h b"))
            nc.sync.dma_start(out=mr_col[H : 2 * H, 0:1], in_=rstd.rearrange("b h -> h b"))
        load_g(1)
        load_w(0, 1)
        load_ha(0, 1)
        load_w(1, 1)
        load_ha(1, 1)
        load_w(2, 2)
        load_ha(2, 2)
        load_w(4, 2)
        load_ha(4, 2)

        mr = kept("mr", [P, 2 * H], F32)
        scale = kept("scale", [P, H, 2], F32)
        scale_mu = kept("scale_mu", [P, H, 2], F32)
        offset = kept("offset", [P, H, 2], F32)
        a_weight = kept("a_weight", [P, H], F32)
        b_weights = kept("b_weights", [P, H, 8], F32)
        nc.vector.memset(b_weights[:], -INV_N)
        wb_t = {}

        def by_group(cols, n):
            return cols.unsqueeze(2).to_broadcast([P, H, n])

        def constants_spread():
            ps = bank("ha", [P, P], F32)
            nc.tensor.transpose(ps[:], wb_rows[:].bitcast(F32), ident[:])
            pairs = ps[:].bitcast(BF16).rearrange("p (r e) -> p r e", e=2)
            wb_t["w"], wb_t["b"] = pairs[:, 0:H, :], pairs[:, H : 2 * H, :]
            mr_ps = bank("hw", [P, P], F32)
            nc.tensor.transpose(mr_ps[:], mr_col[:, 0:1].to_broadcast([P, P]), ident[:])
            nc.vector.tensor_copy(out=mr[:], in_=mr_ps[:, 0 : 2 * H])

        def constants_scale():
            r = mr[:, H : 2 * H]
            nc.vector.tensor_tensor(out=scale[:], in0=wb_t["w"], in1=by_group(r, 2), op=ALU.mult)
            nc.vector.scalar_tensor_tensor(out=a_weight[:], in0=r, scalar=-INV_N, in1=r, op0=ALU.mult, op1=ALU.mult)

        def constants_mu():
            nc.vector.tensor_tensor(out=scale_mu[:], in0=scale[:], in1=by_group(mr[:, 0:H], 2), op=ALU.mult)
            nc.vector.scalar_tensor_tensor(
                out=b_weights[:, :, 4:8],
                in0=by_group(a_weight[:], 4),
                scalar=-1.0,
                in1=by_group(mr[:, 0:H], 4),
                op0=ALU.mult,
                op1=ALU.mult,
            )

        def constants_offset():
            nc.vector.tensor_tensor(out=offset[:], in0=wb_t["b"], in1=scale_mu[:], op=ALU.subtract)

        gf_codes, gf_scales, gf_in = {}, {}, {}
        gt_codes, gt_scales, gt_in = {}, {}, {}
        w_codes, w_scales, w_in = {}, {}, {}
        h_codes, h_scales, pair_in, pair_codes, pair_scales = {}, {}, {}, {}, {}
        ha_t, h_t, dn, sums, totals, coef, shift, dx_ps = {}, {}, {}, {}, {}, {}, {}, {}

        def quantize(codes, scales, values, fmt):
            nc.vector.quantize_mx(out=codes.bitcast(fmt), scales=scales, in_=values)

        def copy_on_vector(out, in_):
            nc.vector.tensor_copy(out=out, in_=in_)

        def copy_on_scalar(out, in_):
            nc.scalar.copy(out=out, in_=in_)

        def transpose_g(G, k, tags):
            gf_in[G, k] = ring("gf_in", [P, 2, 1024], BF16, 2)
            words = g_sb[G, k][:].bitcast(F32)
            for u in range(2):
                ps = bank(tags[u], [P, 4, P], F32)
                for e in range(2):
                    for w in range(2):
                        nc.tensor.transpose(ps[:, 2 * e + w, :], words[:, 2 * e + u, w:256:2], ident[:])
                nc.scalar.copy(
                    out=gf_in[G, k][:, u, :].bitcast(F32).rearrange("p (t m) -> p t m", m=4),
                    in_=ps[:].rearrange("p m t -> p t m"),
                )

        def quantize_gf(G, k):
            gf_codes[G, k] = kept("gf_codes%d_%d" % (G, k), [P, HALF], U32)
            gf_scales[G, k] = kept("gf_scales%d_%d" % (G, k), [P, HALF], U8)
            quantize(gf_codes[G, k][:], gf_scales[G, k][:], gf_in[G, k][:].rearrange("p u n -> p (u n)"), E5M2)

        def interleave_g(m, G, copy, shared=False):
            gt_in[m, G] = ring("pair_in", [P, 1024], BF16, 1) if shared else ring("gt_in", [P, 1024], BF16, 4)
            src = g_sb[G, m // 2][:, :, (m % 2) * 256 : (m % 2 + 1) * 256]
            copy(
                gt_in[m, G][:].rearrange("p (d i u e) -> p d u e i", i=4, u=2, e=2),
                src.rearrange("p (e u) (d i) -> p d u e i", u=2, i=4),
            )

        def quantize_gt(m, G):
            gt_codes[m, G] = kept("gt_codes%d_%d" % (m, G), [P, 256], U32)
            gt_scales[m, G] = kept("gt_scales%d_%d" % (m, G), [P, 256], U8)
            quantize(gt_codes[m, G][:], gt_scales[m, G][:], gt_in[m, G][:], E5M2)

        def w_columns(n):
            return w_sb[n // 2][:, n % 2, :, :]

        def interleave_w_on_vector(n):
            w_in[n] = ring("gt_in", [P, 1024], BF16, 4)
            nc.vector.tensor_copy(
                out=w_in[n][:].rearrange("p (e c i j) -> p c e i j", e=2, i=2, j=4),
                in_=w_columns(n).rearrange("p j (c i e) -> p c e i j", i=2, e=2),
            )

        def quantize_w(n):
            w_codes[n] = kept("w_codes%d" % n, [P, 2 * P], U32)[:]
            w_scales[n] = kept("w_scales%d" % n, [P, 2 * P], U8)[:]
            quantize(w_codes[n], w_scales[n], w_in[n][:], E4M3)

        def open_pair(i):
            pair_in[i] = ring("pair_in", [P, 2, 1024], BF16, 1)

        def h_first(i):
            return (i // 2) % 2

        def interleave_w_on_gpsimd(n, i):
            open_pair(i)
            nc.gpsimd.tensor_scalar(
                out=pair_in[i][:, h_first(i), :].rearrange("p (e c j) -> p c e j", e=2, j=4),
                in0=w_columns(n).rearrange("p j (c e) -> p c e j", e=2),
                scalar1=1.0,
                scalar2=0.0,
                op0=ALU.mult,
                op1=ALU.add,
            )

        def transpose_ha(i, tag):
            ps = bank(tag, [P, 2, 2, P], F32)
            for u in range(2):
                for f in range(2):
                    words = ha_sb[i // 2, u][:, 2 * (i % 2) + f, :].bitcast(F32)
                    nc.tensor.transpose(ps[:, u, f, :], words, ident[:])
            pairs = ps[:].rearrange("p u f q -> p (u f q)").bitcast(BF16).rearrange("p (n e) -> p n e", e=2)
            ha_t[i] = [pairs[:, :, e] for e in range(2)]

        def make_h(i, parities_on_scalar):
            h_t[i] = ring("h_t", [P, 2, HALF], BF16, 2)
            for e in range(2):
                mul, add = scale[:, i // 2, e : e + 1], offset[:, i // 2, e : e + 1]
                if e < parities_on_scalar:
                    nc.scalar.activation(out=h_t[i][:, e, :], in_=ha_t[i][e], func=IDENTITY, scale=mul, bias=add)
                else:
                    nc.vector.tensor_scalar(
                        out=h_t[i][:, e, :], in0=ha_t[i][e], scalar1=mul, scalar2=add, op0=ALU.mult, op1=ALU.add
                    )

        def transpose_h(i):
            ps = bank("hw", [P, 2, 2, P], F32)
            for e in range(2):
                words = h_t[i][:, e, :].bitcast(F32)
                for u in range(2):
                    nc.tensor.transpose(ps[:, e, u, :], words[:, u * P : (u + 1) * P], ident[:])
            if i not in pair_in:
                open_pair(i)
            nc.scalar.copy(
                out=pair_in[i][:, 1 - h_first(i), :].bitcast(F32).rearrange("p (e c u) -> p e c u", e=2, u=2),
                in_=ps[:].rearrange("p e u c -> p e c u"),
            )

        def quantize_pair(i, n=None):
            chunk, second, G = i // 4, h_first(i), i % 2
            if not second:
                pair_codes[chunk, G] = ring("pair_codes%d" % G, [P, 4, DH], U32, 2)
                pair_scales[chunk, G] = ring("pair_scales%d" % G, [P, 4, DH], U8, 2)
                h_codes[chunk, G] = pair_codes[chunk, G][:, 1:3, :].rearrange("p a c -> p (a c)")
                h_scales[chunk, G] = pair_scales[chunk, G][:, 1:3, :].rearrange("p a c -> p (a c)")
            codes, scales = pair_codes[chunk, G], pair_scales[chunk, G]
            if n is None:
                quantize(codes[:, 1 + second, :], scales[:, 1 + second, :], pair_in[i][:, 1 - second, :], E4M3)
            else:
                w_codes[n], w_scales[n] = codes[:, 3 * second, :], scales[:, 3 * second, :]
                both = slice(2 * second, 2 * second + 2)
                quantize(
                    codes[:, both, :].rearrange("p a c -> p (a c)"),
                    scales[:, both, :].rearrange("p a c -> p (a c)"),
                    pair_in[i][:].rearrange("p a c -> p (a c)"),
                    E4M3,
                )

        def product_dh(i, e):
            group, G = divmod(i, 2)
            if e == 0:
                if G == 0:
                    sums[group] = ring("sums", [P, 8], F32, 2)
                dn[i] = ring("dn", [P, 2, HALF], F32, 4)
            ps = bank("dh%d" % e, [P, HALF], F32)
            for k in range(2):
                n = 2 * group + k
                nc.tensor.matmul_mx(
                    out=ps[:],
                    lhsT=w_codes[n][:, e * P : (e + 1) * P].bitcast(E4M3),
                    lhsT_scale=w_scales[n][:, e * P : (e + 1) * P],
                    rhs=gf_codes[G, k][:].bitcast(E5M2),
                    rhs_scale=gf_scales[G, k][:],
                    start=(k == 0),
                    stop=(k == 1),
                )
            nc.scalar.activation(
                out=dn[i][:, e, :],
                in_=ps[:],
                func=IDENTITY,
                scale=scale[:, group, e : e + 1],
                accum_out=sums[group][:, 2 * G + e : 2 * G + e + 1],
            )

        def product_dw(chunk, m, tags, store_each=False, between=None):
            stage = ring("dw_stage", [P, 2, CHUNK], F32, 5)
            rows = out_1[256 * m : 256 * (m + 1), chunk * CHUNK : (chunk + 1) * CHUNK]
            rows = rows.rearrange("(t p) c -> p t c", p=P)
            tiles = [bank(tag, [P, CHUNK], F32) for tag in tags]
            for t in range(2):
                for G in range(2):
                    nc.tensor.matmul_mx(
                        out=tiles[t][:],
                        lhsT=gt_codes[m, G][:, t * P : (t + 1) * P].bitcast(E5M2),
                        lhsT_scale=gt_scales[m, G][:, t * P : (t + 1) * P],
                        rhs=h_codes[chunk, G].bitcast(E4M3),
                        rhs_scale=h_scales[chunk, G],
                        start=(G == 0),
                        stop=(G == 1),
                    )
            for t in range(2):
                nc.scalar.copy(
                    out=stage[:, t, :].rearrange("p (g c e) -> p g c e", g=2, e=2),
                    in_=tiles[t][:].rearrange("p (g e c) -> p g c e", g=2, e=2),
                )
                if store_each:
                    nc.sync.dma_start(out=rows[:, t, :], in_=stage[:, t, :])
                if between and t == 0:
                    between()
            if not store_each:
                nc.sync.dma_start(out=rows, in_=stage[:])

        def sum_dn_ha(i, e):
            group, G = divmod(i, 2)
            products = ring("products", [P, HALF], F32, 2)
            nc.vector.scalar_tensor_tensor(
                out=products[:],
                in0=ha_t[i][e],
                scalar=mr[:, group : group + 1],
                in1=dn[i][:, e, :],
                op0=ALU.subtract,
                op1=ALU.mult,
                accum_out=sums[group][:, 4 + 2 * G + e : 5 + 2 * G + e],
            )

        def group_totals(group, tag):
            totals[group] = bank(tag, [P, 8], F32)
            nc.tensor.matmul(out=totals[group][:], lhsT=ones[:], rhs=sums[group][:], start=True, stop=True)

        def group_coefficients(group):
            coef[group] = ring("coef", [P, 2], F32, 2)
            terms = ring("terms", [P, 12], F32, 2)
            nc.vector.tensor_scalar(
                out=terms[:, 0:4],
                in0=totals[group][:, 4:8],
                scalar1=a_weight[:, group : group + 1],
                scalar2=None,
                op0=ALU.mult,
                op1=ALU.add,
                accum_out=coef[group][:, 0:1],
            )
            nc.vector.scalar_tensor_tensor(
                out=terms[:, 4:12],
                in0=totals[group][:],
                scalar=1.0,
                in1=b_weights[:, group, :],
                op0=ALU.mult,
                op1=ALU.mult,
                accum_out=coef[group][:, 1:2],
            )

        def make_shift(i, u, on_scalar=False):
            group, G = divmod(i, 2)
            shift[i, u] = ring("shift", [P, 2, DH], F32, 6)
            src, a, b = ha_sb[group, u][:, 2 * G : 2 * G + 2, :], coef[group][:, 0:1], coef[group][:, 1:2]
            if on_scalar:
                nc.scalar.activation(out=shift[i, u][:], in_=src, func=IDENTITY, scale=a, bias=b)
            else:
                nc.gpsimd.tensor_scalar(
                    out=shift[i, u][:], in0=src, scalar1=a, scalar2=b, op0=ALU.mult, op1=ALU.add
                )

        def transpose_dn(i, u, tag):
            dx_ps[i, u] = bank(tag, [P, 2, 2, P], F32)
            for f in range(2):
                for e in range(2):
                    t0 = u * 256 + f * P
                    nc.tensor.transpose(dx_ps[i, u][:, f, e, :], dn[i][:, e, t0 : t0 + P], ident[:])

        def finish_dx(i, u):
            group, G = divmod(i, 2)
            stage = ring("dx_stage", [P, 2, DH], F32, 8)
            nc.vector.tensor_tensor(
                out=stage[:].rearrange("p f (c e) -> p f c e", e=2),
                in0=dx_ps[i, u][:].rearrange("p f e c -> p f c e"),
                in1=shift[i, u][:].rearrange("p f (c e) -> p f c e", e=2),
                op=ALU.add,
            )
            nc.sync.dma_start(out=dx_hbm[:, u, 2 * G : 2 * G + 2, group * DH : (group + 1) * DH], in_=stage[:])

        interleave_g(0, 0, copy_on_scalar)
        interleave_g(1, 0, copy_on_vector)
        transpose_g(0, 0, ("dx0", "dx1"))
        interleave_g(2, 0, copy_on_scalar)
        quantize_gt(1, 0)
        interleave_g(3, 0, copy_on_vector)
        quantize_gt(0, 0)
        constants_spread()
        quantize_gt(3, 0)
        constants_scale()
        transpose_g(0, 1, ("dw0", "dw1"))
        quantize_gf(0, 0)
        constants_mu()
        interleave_g(0, 1, copy_on_vector)
        constants_offset()
        quantize_gt(2, 0)
        interleave_g(1, 1, copy_on_vector)
        quantize_gt(0, 1)
        quantize_gf(0, 1)
        quantize_gt(1, 1)
        transpose_g(1, 0, ("dx0", "dx1"))
        interleave_w_on_vector(0)
        interleave_w_on_vector(1)
        quantize_w(0)
        quantize_w(1)
        transpose_g(1, 1, ("ha", "hw"))
        transpose_ha(0, "dw0")
        quantize_gf(1, 0)
        interleave_g(2, 1, copy_on_vector)
        quantize_gf(1, 1)

        late_loads = {3: load_w, 4: load_ha}
        last = STEPS - 1

        for i in range(STEPS):
            early = i < DW_LAG
            stats = i >= 2 and i % 2 == 0
            if i in late_loads:
                late_loads[i](6, 2)
            if i == 0:
                interleave_g(3, 1, copy_on_vector, True)
                quantize_gt(2, 1)
                interleave_w_on_vector(3)
                quantize_gt(3, 1)
                interleave_w_on_gpsimd(2, 0)
            if i == 1:
                quantize_w(3)
                quantize_pair(0, 2)
            if 2 <= i < STEPS - 3:
                quantize_pair(i - 1, i + 2)
            if 1 <= i < STEPS - 3:
                interleave_w_on_gpsimd(i + 3, i)
            if i >= 3:
                finish_dx(i - 3, 1)
            make_h(i, 2 if early else 1)
            if i >= STEPS - 3:
                quantize_pair(i - 1, i + 2 if i + 2 < STEPS else None)
            product_dh(i, 0)
            product_dh(i, 1)
            if stats:
                group_totals(i // 2 - 1, "hw")
            if not early:
                between = (lambda: transpose_h(last)) if i == last else None
                product_dw((i - DW_LAG) // 4, (i - DW_LAG) % 4, ("dw0", "dw1"), i == last, between)
            if stats:
                group_coefficients(i // 2 - 1)
            sum_dn_ha(i, 0)
            if i >= 2:
                for u in range(2):
                    make_shift(i - 2, u, early and u == 0)
            sum_dn_ha(i, 1)
            if early:
                transpose_ha(i + 1, "dw%d" % ((i + 1) % 2) if i + 1 < DW_LAG else "ha")
            if i < last:
                transpose_h(i)
            if i >= 2:
                for u in range(2):
                    transpose_dn(i - 2, u, "dx%d" % u)
                finish_dx(i - 2, 0)
            if not early and i < last:
                transpose_ha(i + 1, "ha")

        quantize_pair(last)
        for u in range(2):
            transpose_dn(last - 1, u, "dh%d" % u)
        group_totals(H - 1, "ha")
        group_coefficients(H - 1)
        finish_dx(last - 2, 1)
        for i in (last - 1, last):
            for u in range(2):
                make_shift(i, u)
        product_dw(3, 0, ("dw0", "dw1"), True)
        for u in range(2):
            finish_dx(last - 1, u)
        product_dw(3, 1, ("ha", "dx1"))
        for u in range(2):
            transpose_dn(last, u, ("hw", "dx0")[u])
            finish_dx(last, u)
        product_dw(3, 2, ("dw0", "dw1"))
        product_dw(3, 3, ("dh0", "dh1"), store_each=True)
